import numpy as np
import ml_dtypes


def mxq(x, axis, fmt="e4m3"):
    dtype, down = {"e4m3": (ml_dtypes.float8_e4m3fn, 7), "e5m2": (ml_dtypes.float8_e5m2, 14)}[fmt]
    v = np.moveaxis(np.asarray(x, np.float32).astype(ml_dtypes.bfloat16).astype(np.float64), axis, -1)
    blocks = v.reshape(v.shape[:-1] + (-1, 32))
    amax = np.abs(blocks).max(-1, keepdims=True)
    byte = np.maximum(np.where(amax > 0, np.frexp(amax)[1] - 1 + 127, 0) - down, 1)
    scale = np.exp2(byte - 127.0)
    codes = (blocks / scale).astype(np.float32).astype(dtype).astype(np.float64)
    return np.moveaxis((codes * scale).reshape(v.shape), -1, axis)


WIDE = False


def mx_kscale(k):
    if not WIDE:
        return np.ones(k)
    levels = np.array([10, -10, 5, -5, 0])
    a = np.random.permutation(np.resize(levels, k // 512 * 4)).reshape(k // 512, 4)
    idx = np.arange(k)
    return np.exp2(a[idx // 512, idx % 128 // 32])


BF16 = ml_dtypes.bfloat16


def bf(x):
    return np.asarray(x, np.float32).astype(BF16)


def f64(x):
    return np.asarray(x).astype(np.float64)


E2M1 = np.array([0.0, 0.5, 1.0, 1.5, 2.0, 3.0, 4.0, 6.0, -0.0, -0.5, -1.0, -1.5, -2.0, -3.0, -4.0, -6.0])


def pack_weight(w, fmt):
    k, n = w.shape
    w = f64(bf(w)).reshape(k // 32, 32, n)
    amax = np.abs(w).max(1)
    if fmt == "e4m3":
        byte = np.frexp(amax)[1] - 1 + 127 - 7
    else:
        mant, ex = np.frexp(amax / 6.0)
        byte = np.where(mant > 0.5, ex, ex - 1) + 127
    byte = np.clip(np.where(amax > 0, byte, 1), 1, 254)
    scaled = (w * np.exp2(127.0 - byte)[:, None, :]).reshape(k, n).astype(np.float32)
    by_word = np.ascontiguousarray(scaled.reshape(k // 512, 128, 4, n).transpose(0, 1, 3, 2))
    if fmt == "e4m3":
        words = by_word.astype(ml_dtypes.float8_e4m3fn).view(np.uint8)
    else:
        c = by_word.astype(ml_dtypes.float4_e2m1fn).view(np.uint8) & 0xF
        words = c[..., 0::2] | (c[..., 1::2] << 4)
    return np.ascontiguousarray(words), np.ascontiguousarray(byte.astype(np.uint8).reshape(k // 512, 16, n))


def unpack_weight(words, scales, fmt):
    g, p, n, _ = words.shape
    if fmt == "e4m3":
        vals = np.ascontiguousarray(words).view(ml_dtypes.float8_e4m3fn).astype(np.float64)
    else:
        nib = np.empty((g, p, n, 4), np.uint8)
        nib[..., 0::2] = words & 0xF
        nib[..., 1::2] = words >> 4
        vals = E2M1[nib]
    vals = vals * np.repeat(np.exp2(scales.astype(np.float64) - 127.0), 8, axis=1)[..., None]
    return vals.transpose(0, 1, 3, 2).reshape(g * 512, n)


B, N, CIN, COUT = 8, 512, 1024, 512
NW = 2


def xavier():
    return np.random.uniform(-1.0, 1.0, (CIN, COUT)) * (1.414 * np.sqrt(6.0 / (CIN + COUT)))


def setup_inputs():
    s = mx_kscale(CIN)
    x = bf(np.random.standard_normal((B, N, CIN)) * s)
    stack = np.stack([xavier(), xavier()]) / s[None, :, None]
    W_words, W_scales = pack_weight(stack.reshape(-1, COUT), "e4m3")
    return {"x": x,
            "W_words": W_words,
            "W_scales": W_scales,
            "M": bf(1.0 + 0.1 * np.random.standard_normal((N, COUT))),
            "adj": bf(np.random.uniform(0.0, 1.0, (N, N)) * 1.5 / np.sqrt(N) + np.eye(N) * np.random.uniform(0.5, 1.5, (N, 1))),
            "adj2": bf(np.random.standard_normal((N, N)) * 0.5 / np.sqrt(N)),
            "bias": bf(np.random.standard_normal(COUT) * 0.5)}


def reference(x, W_words, W_scales, M, adj, adj2, bias):
    xq = mxq(f64(x), 2, "e4m3")
    Wf = unpack_weight(W_words, W_scales, "e4m3").reshape(NW, CIN, COUT)
    h0 = xq @ Wf[0]
    h1 = xq @ Wf[1]
    A = f64(adj) + f64(adj2)
    A = (A.T + A) * 0.5
    E = np.eye(N)
    a_self = np.diagonal(A)
    a_off = A * (1.0 - E)
    g0 = f64(M) * h0
    g1 = f64(M) * h1
    agg = mxq(a_off, 1, "e4m3") @ mxq(g1, 1, "e4m3")
    return a_self[None, :, None] * g0 + agg + f64(bias)

@@ -1,0 +1,217 @@
+from contextlib import ExitStack
+
+import concourse.mybir as mybir
+from concourse.masks import make_identity
+
+F32 = mybir.dt.float32
+BF16 = mybir.dt.bfloat16
+I32 = mybir.dt.int32
+U32 = mybir.dt.uint32
+U8 = mybir.dt.uint8
+FP8X4 = mybir.dt.float8_e4m3fn_x4
+ADD = mybir.AluOpType.add
+SUBTRACT = mybir.AluOpType.subtract
+MULT = mybir.AluOpType.mult
+COPY = mybir.ActivationFunctionType.Copy
+
+P = 128
+PACK = 4
+K_PASS = P * PACK
+BATCH = 8
+NODES = 512
+CIN = 1024
+COUT = 512
+X_PASSES = CIN // K_PASS
+TILES = NODES // P
+
+FLOPS = 2 * BATCH * NODES * CIN * COUT * 2 + 2 * BATCH * NODES * NODES * COUT
+
+
+def tile_modulatedgraphconv_pa_t_e_kernel(tc, x, W_words, W_scales, M, adj, adj2, bias, out):
+    nc = tc.nc
+    with ExitStack() as ctx:
+        const = ctx.enter_context(tc.tile_pool(name="const", bufs=1))
+        x_pool = ctx.enter_context(tc.tile_pool(name="x_pool", bufs=BATCH))
+        xg_pool = ctx.enter_context(tc.tile_pool(name="xg_pool", bufs=2))
+        xq_pool = ctx.enter_context(tc.tile_pool(name="xq_pool", bufs=2))
+        g_pool = ctx.enter_context(tc.tile_pool(name="g_pool", bufs=2))
+        o_pool = ctx.enter_context(tc.tile_pool(name="o_pool", bufs=3))
+        psum_xt = ctx.enter_context(tc.psum_pool(name="psum_xt", bufs=2))
+        psum_acc = ctx.enter_context(tc.psum_pool(name="psum_acc", bufs=6))
+
+        w_scales = const.tile([P, 2 * X_PASSES, COUT], U8, align_bytes=64)
+        nc.vector.memset(w_scales[:].bitcast(I32), 0)
+        for quadrant in range(4):
+            nc.sync.dma_start(
+                out=w_scales[:].bitcast(I32)[32 * quadrant : 32 * quadrant + 4, :, :],
+                in_=W_scales.bitcast(I32)[:, 4 * quadrant : 4 * quadrant + 4, :].rearrange("g r n -> r g n"),
+            )
+        adj_sb = const.tile([P, TILES, NODES], BF16)
+        adj2_sb = const.tile([P, TILES, NODES], BF16)
+        nc.sync.dma_start(out=adj_sb[:], in_=adj.rearrange("(p t) i -> p t i", t=TILES))
+        nc.sync.dma_start(out=adj2_sb[:], in_=adj2.rearrange("(p t) i -> p t i", t=TILES))
+        x_sb = [x_pool.tile([P, TILES, CIN], BF16, name="x_sb") for b in range(BATCH)]
+        nc.sync.dma_start(out=x_sb[0][:], in_=x[0].rearrange("(p t) k -> p t k", t=TILES))
+        m_sb = const.tile([P, TILES, COUT], BF16)
+        nc.sync.dma_start(out=m_sb[:], in_=M.rearrange("(p t) c -> p t c", t=TILES))
+        w_words = const.tile([P, 2 * X_PASSES, PACK * COUT], U8, align_bytes=64)
+        for g in range(2 * X_PASSES):
+            nc.sync.dma_start(
+                out=w_words[:, g, :].bitcast(I32),
+                in_=W_words[g].rearrange("p n t -> p (n t)").bitcast(I32),
+            )
+        for b in range(1, BATCH):
+            nc.sync.dma_start(out=x_sb[b][:], in_=x[b].rearrange("(p t) k -> p t k", t=TILES))
+        bias_bf = const.tile([P, COUT], BF16)
+        nc.gpsimd.dma_start(out=bias_bf[:], in_=bias.partition_broadcast(P))
+        ident = const.tile([P, P], F32)
+        make_identity(nc, ident[:])
+
+        adj2_half = const.tile([P, TILES, NODES], BF16)
+        nc.scalar.mul(out=adj2_half[:], in_=adj2_sb[:], mul=0.5)
+        s_half = const.tile([P, TILES * TILES, P], F32)
+        for t in range(TILES):
+            nc.vector.scalar_tensor_tensor(
+                out=s_half[:, TILES * t : TILES * (t + 1), :],
+                in0=adj_sb[:, t, :].rearrange("p (m t2) -> p t2 m", t2=TILES),
+                scalar=0.5,
+                in1=adj2_half[:, t, :].rearrange("p (m t2) -> p t2 m", t2=TILES),
+                op0=MULT,
+                op1=ADD,
+            )
+        diag_blocks = s_half[:, 0 : TILES * TILES : TILES + 1, :]
+        diag_part = const.tile([P, TILES, P], F32)
+        nc.vector.tensor_tensor(
+            out=diag_part[:], in0=diag_blocks, in1=ident[:].unsqueeze(1).to_broadcast([P, TILES, P]), op=MULT
+        )
+        diag_half = const.tile([P, TILES], F32)
+        nc.vector.tensor_reduce(out=diag_half[:], in_=diag_part[:], axis=mybir.AxisListType.X, op=ADD)
+        a_self = const.tile([P, TILES], F32)
+        nc.vector.tensor_scalar_mul(out=a_self[:], in0=diag_half[:], scalar1=2.0)
+        nc.vector.tensor_tensor(out=diag_blocks, in0=diag_blocks, in1=diag_part[:], op=SUBTRACT)
+        a_grouped = const.tile([P, NODES, PACK], BF16, align_bytes=64)
+        for t2 in range(TILES):
+            flipped = psum_acc.tile([P, TILES, P], F32, name="flipped", tag="acc")
+            for t in range(TILES):
+                nc.tensor.transpose(flipped[:, t, :], s_half[:, TILES * t2 + t, :], ident[:])
+            nc.vector.tensor_tensor(
+                out=a_grouped[:, P * t2 : P * (t2 + 1), :],
+                in0=flipped[:].rearrange("p t m -> p m t"),
+                in1=s_half[:, t2 : TILES * TILES : TILES, :].rearrange("p t m -> p m t"),
+                op=ADD,
+            )
+        a_codes = const.tile([P, NODES], U32, align_bytes=64)
+        a_scales = const.tile([P, NODES], U8, align_bytes=64)
+
+        ms = const.tile([P, TILES, COUT], F32)
+        m_grouped = const.tile([P, COUT, PACK], BF16)
+        bias_f32 = const.tile([P, COUT], F32)
+
+        def transpose_x(b):
+            xg = xg_pool.tile([P, X_PASSES, PACK * NODES], BF16, name="xg", align_bytes=64)
+            for g in range(X_PASSES):
+                xg_words = xg[:, g, :].bitcast(F32).rearrange("p (n u) -> p n u", u=2)
+                for half in range(2):
+                    xt = psum_xt.tile([P, 2, 2 * P], F32, name="xt")
+                    for tt in range(2):
+                        words = x_sb[b][:, 2 * half + tt, :].bitcast(F32)
+                        for u in range(2):
+                            nc.tensor.transpose(
+                                xt[:, u, P * tt : P * (tt + 1)],
+                                words[:, 256 * g + u : 256 * (g + 1) : 2],
+                                ident[:],
+                            )
+                    nc.scalar.copy(
+                        out=xg_words[:, 2 * P * half : 2 * P * (half + 1), :],
+                        in_=xt[:].rearrange("p u n -> p n u"),
+                    )
+            return xg
+
+        def quantise_x(xg):
+            x_codes = xq_pool.tile([P, X_PASSES, NODES], U32, name="x_codes", align_bytes=64)
+            x_scales = xq_pool.tile([P, X_PASSES, NODES], U8, name="x_scales", align_bytes=64)
+            for g in range(X_PASSES):
+                nc.vector.quantize_mx(
+                    out=x_codes[:, g, :].bitcast(FP8X4), scales=x_scales[:, g, :], in_=xg[:, g, :]
+                )
+            return x_codes, x_scales
+
+        def project(acc, xq, t, which, c0, width):
+            x_codes, x_scales = xq
+            nodes = slice(P * t, P * (t + 1))
+            for g in range(X_PASSES):
+                wg = X_PASSES * which + g
+                nc.tensor.matmul_mx(
+                    out=acc,
+                    lhsT=x_codes[:, g, nodes].bitcast(FP8X4),
+                    lhsT_scale=x_scales[:, g, nodes],
+                    rhs=w_words[:, wg, PACK * c0 : PACK * (c0 + width)].bitcast(FP8X4),
+                    rhs_scale=w_scales[:, wg, c0 : c0 + width],
+                    start=(g == 0),
+                    stop=(g == X_PASSES - 1),
+                )
+
+        def self_term(xq):
+            o_sb = o_pool.tile([P, TILES, COUT], F32, name="o_sb")
+            for t in range(TILES):
+                h0 = psum_acc.tile([P, COUT], F32, name="h0", tag="acc")
+                project(h0[:], xq, t, 0, 0, COUT)
+                nc.vector.tensor_tensor(out=o_sb[:, t, :], in0=h0[:], in1=ms[:, t, :], op=MULT)
+                nc.gpsimd.tensor_tensor(out=o_sb[:, t, :], in0=o_sb[:, t, :], in1=bias_f32[:], op=ADD)
+            return o_sb
+
+        def neighbour_operand(xq):
+            g1 = g_pool.tile([P, COUT, PACK], BF16, name="g1", align_bytes=64)
+            for s in range(COUT // P):
+                cols = slice(P * s, P * (s + 1))
+                h1 = psum_acc.tile([P, TILES, P], F32, name="h1", tag="acc")
+                for t in range(TILES):
+                    project(h1[:, t, :], xq, t, 1, P * s, P)
+                nc.vector.tensor_tensor(
+                    out=g1[:, cols, :], in0=h1[:].rearrange("p t c -> p c t"), in1=m_grouped[:, cols, :], op=MULT
+                )
+            g_codes = g_pool.tile([P, COUT], U32, name="g_codes", align_bytes=64)
+            g_scales = g_pool.tile([P, COUT], U8, name="g_scales", align_bytes=64)
+            nc.vector.quantize_mx(
+                out=g_codes[:].bitcast(FP8X4), scales=g_scales[:], in_=g1[:].rearrange("p c t -> p (c t)")
+            )
+            return g_codes, g_scales
+
+        def aggregate_and_store(b, gq, o_sb):
+            g_codes, g_scales = gq
+            out_b = out[b].rearrange("(p t) c -> p t c", t=TILES)
+            for t in range(TILES):
+                nodes = slice(P * t, P * (t + 1))
+                agg = psum_acc.tile([P, COUT], F32, name="agg", tag="acc")
+                nc.tensor.matmul_mx(
+                    out=agg[:],
+                    lhsT=a_codes[:, nodes].bitcast(FP8X4),
+                    lhsT_scale=a_scales[:, nodes],
+                    rhs=g_codes[:].bitcast(FP8X4),
+                    rhs_scale=g_scales[:],
+                    start=True,
+                    stop=True,
+                )
+                nc.vector.tensor_tensor(out=o_sb[:, t, :], in0=agg[:], in1=o_sb[:, t, :], op=ADD)
+                if t % 2 == 1:
+                    nc.sync.dma_start(out=out_b[:, t - 1 : t + 1, :], in_=o_sb[:, t - 1 : t + 1, :])
+
+        xq = {0: quantise_x(transpose_x(0))}
+        for t in range(TILES):
+            nc.scalar.activation(out=ms[:, t, :], in_=m_sb[:, t, :], func=COPY, scale=a_self[:, t : t + 1])
+        nc.scalar.copy(out=bias_f32[:], in_=bias_bf[:])
+        nc.scalar.copy(out=m_grouped[:], in_=m_sb[:].rearrange("p t c -> p c t"))
+        nc.vector.quantize_mx(
+            out=a_codes[:].bitcast(FP8X4), scales=a_scales[:], in_=a_grouped[:].rearrange("p w t -> p (w t)")
+        )
+        gq = {}
+        o_tiles = {}
+        for b in range(BATCH + 1):
+            if b < BATCH:
+                o_tiles[b] = self_term(xq[b])
+            if b >= 1:
+                aggregate_and_store(b - 1, gq[b - 1], o_tiles[b - 1])
+            if b + 1 < BATCH:
+                xq[b + 1] = quantise_x(transpose_x(b + 1))
+            if b < BATCH:
+                gq[b] = neighbour_operand(xq[b])

@@ -10,7 +10,6 @@ U32 = mybir.dt.uint32
 U8 = mybir.dt.uint8
 FP8X4 = mybir.dt.float8_e4m3fn_x4
 ADD = mybir.AluOpType.add
-SUBTRACT = mybir.AluOpType.subtract
 MULT = mybir.AluOpType.mult
 COPY = mybir.ActivationFunctionType.Copy
 
@@ -23,6 +22,8 @@ CIN = 1024
 COUT = 512
 X_PASSES = CIN // K_PASS
 TILES = NODES // P
+HALF = NODES // 2
+AHEAD = 2
 
 FLOPS = 2 * BATCH * NODES * CIN * COUT * 2 + 2 * BATCH * NODES * NODES * COUT
 
@@ -33,11 +34,25 @@ def tile_modulatedgraphconv_pa_t_e_kernel(tc, x, W_words, W_scales, M, adj, adj2
         const = ctx.enter_context(tc.tile_pool(name="const", bufs=1))
         x_pool = ctx.enter_context(tc.tile_pool(name="x_pool", bufs=BATCH))
         xg_pool = ctx.enter_context(tc.tile_pool(name="xg_pool", bufs=2))
-        xq_pool = ctx.enter_context(tc.tile_pool(name="xq_pool", bufs=2))
+        xq_pool = ctx.enter_context(tc.tile_pool(name="xq_pool", bufs=AHEAD + 1))
         g_pool = ctx.enter_context(tc.tile_pool(name="g_pool", bufs=2))
         o_pool = ctx.enter_context(tc.tile_pool(name="o_pool", bufs=3))
-        psum_xt = ctx.enter_context(tc.psum_pool(name="psum_xt", bufs=2))
-        psum_acc = ctx.enter_context(tc.psum_pool(name="psum_acc", bufs=6))
+        psum_xt = ctx.enter_context(tc.psum_pool(name="psum_xt", bufs=3))
+        psum_acc = ctx.enter_context(tc.psum_pool(name="psum_acc", bufs=5))
+        ctx.enter_context(tc.manual_schedule())
+
+        diag_adj = const.tile([P, TILES], BF16)
+        diag_adj2 = const.tile([P, TILES], BF16)
+        with nc.allow_non_contiguous_dma(reason="the 512 diagonal elements of a matrix"):
+            for diag_sb, matrix in ((diag_adj, adj), (diag_adj2, adj2)):
+                nc.scalar.dma_start(
+                    out=diag_sb[:],
+                    in_=matrix.rearrange("i j -> (i j)")[0 : NODES * NODES : NODES + 1].rearrange(
+                        "(p t) -> p t", t=TILES
+                    ),
+                )
+        bias_bf = const.tile([P, COUT], BF16)
+        nc.gpsimd.dma_start(out=bias_bf[:], in_=bias.partition_broadcast(P))
 
         w_scales = const.tile([P, 2 * X_PASSES, COUT], U8, align_bytes=64)
         nc.vector.memset(w_scales[:].bitcast(I32), 0)
@@ -46,12 +61,15 @@ def tile_modulatedgraphconv_pa_t_e_kernel(tc, x, W_words, W_scales, M, adj, adj2
                 out=w_scales[:].bitcast(I32)[32 * quadrant : 32 * quadrant + 4, :, :],
                 in_=W_scales.bitcast(I32)[:, 4 * quadrant : 4 * quadrant + 4, :].rearrange("g r n -> r g n"),
             )
-        adj_sb = const.tile([P, TILES, NODES], BF16)
-        adj2_sb = const.tile([P, TILES, NODES], BF16)
-        nc.sync.dma_start(out=adj_sb[:], in_=adj.rearrange("(p t) i -> p t i", t=TILES))
-        nc.sync.dma_start(out=adj2_sb[:], in_=adj2.rearrange("(p t) i -> p t i", t=TILES))
         x_sb = [x_pool.tile([P, TILES, CIN], BF16, name="x_sb") for b in range(BATCH)]
-        nc.sync.dma_start(out=x_sb[0][:], in_=x[0].rearrange("(p t) k -> p t k", t=TILES))
+
+        def load_x(b):
+            x_b = x[b].rearrange("(p t) k -> p t k", t=TILES)
+            for half in range(2):
+                tiles = slice(2 * half, 2 * half + 2)
+                nc.sync.dma_start(out=x_sb[b][:, tiles, :], in_=x_b[:, tiles, :])
+
+        load_x(0)
         m_sb = const.tile([P, TILES, COUT], BF16)
         nc.sync.dma_start(out=m_sb[:], in_=M.rearrange("(p t) c -> p t c", t=TILES))
         w_words = const.tile([P, 2 * X_PASSES, PACK * COUT], U8, align_bytes=64)
@@ -60,59 +78,25 @@ def tile_modulatedgraphconv_pa_t_e_kernel(tc, x, W_words, W_scales, M, adj, adj2
                 out=w_words[:, g, :].bitcast(I32),
                 in_=W_words[g].rearrange("p n t -> p (n t)").bitcast(I32),
             )
+        adj_sb = const.tile([P, TILES, NODES], BF16)
+        adj2_sb = const.tile([P, TILES, NODES], BF16)
+        nc.sync.dma_start(out=adj2_sb[:], in_=adj2.rearrange("(p t) i -> p t i", t=TILES))
+        nc.sync.dma_start(out=adj_sb[:], in_=adj.rearrange("(p t) i -> p t i", t=TILES))
         for b in range(1, BATCH):
-            nc.sync.dma_start(out=x_sb[b][:], in_=x[b].rearrange("(p t) k -> p t k", t=TILES))
-        bias_bf = const.tile([P, COUT], BF16)
-        nc.gpsimd.dma_start(out=bias_bf[:], in_=bias.partition_broadcast(P))
+            load_x(b)
+
         ident = const.tile([P, P], F32)
         make_identity(nc, ident[:])
-
-        adj2_half = const.tile([P, TILES, NODES], BF16)
-        nc.scalar.mul(out=adj2_half[:], in_=adj2_sb[:], mul=0.5)
-        s_half = const.tile([P, TILES * TILES, P], F32)
-        for t in range(TILES):
-            nc.vector.scalar_tensor_tensor(
-                out=s_half[:, TILES * t : TILES * (t + 1), :],
-                in0=adj_sb[:, t, :].rearrange("p (m t2) -> p t2 m", t2=TILES),
-                scalar=0.5,
-                in1=adj2_half[:, t, :].rearrange("p (m t2) -> p t2 m", t2=TILES),
-                op0=MULT,
-                op1=ADD,
-            )
-        diag_blocks = s_half[:, 0 : TILES * TILES : TILES + 1, :]
-        diag_part = const.tile([P, TILES, P], F32)
-        nc.vector.tensor_tensor(
-            out=diag_part[:], in0=diag_blocks, in1=ident[:].unsqueeze(1).to_broadcast([P, TILES, P]), op=MULT
+        off_diagonal = const.tile([P, P], F32)
+        nc.gpsimd.tensor_scalar(
+            out=off_diagonal[:], in0=ident[:], scalar1=-1.0, scalar2=1.0, op0=MULT, op1=ADD
         )
-        diag_half = const.tile([P, TILES], F32)
-        nc.vector.tensor_reduce(out=diag_half[:], in_=diag_part[:], axis=mybir.AxisListType.X, op=ADD)
-        a_self = const.tile([P, TILES], F32)
-        nc.vector.tensor_scalar_mul(out=a_self[:], in0=diag_half[:], scalar1=2.0)
-        nc.vector.tensor_tensor(out=diag_blocks, in0=diag_blocks, in1=diag_part[:], op=SUBTRACT)
-        a_grouped = const.tile([P, NODES, PACK], BF16, align_bytes=64)
-        for t2 in range(TILES):
-            flipped = psum_acc.tile([P, TILES, P], F32, name="flipped", tag="acc")
-            for t in range(TILES):
-                nc.tensor.transpose(flipped[:, t, :], s_half[:, TILES * t2 + t, :], ident[:])
-            nc.vector.tensor_tensor(
-                out=a_grouped[:, P * t2 : P * (t2 + 1), :],
-                in0=flipped[:].rearrange("p t m -> p m t"),
-                in1=s_half[:, t2 : TILES * TILES : TILES, :].rearrange("p t m -> p m t"),
-                op=ADD,
-            )
-        a_codes = const.tile([P, NODES], U32, align_bytes=64)
-        a_scales = const.tile([P, NODES], U8, align_bytes=64)
-
-        ms = const.tile([P, TILES, COUT], F32)
-        m_grouped = const.tile([P, COUT, PACK], BF16)
-        bias_f32 = const.tile([P, COUT], F32)
 
         def transpose_x(b):
             xg = xg_pool.tile([P, X_PASSES, PACK * NODES], BF16, name="xg", align_bytes=64)
-            for g in range(X_PASSES):
-                xg_words = xg[:, g, :].bitcast(F32).rearrange("p (n u) -> p n u", u=2)
-                for half in range(2):
-                    xt = psum_xt.tile([P, 2, 2 * P], F32, name="xt")
+            for half in range(2):
+                for g in range(X_PASSES):
+                    xt = psum_xt.tile([P, 2, HALF], F32, name="xt")
                     for tt in range(2):
                         words = x_sb[b][:, 2 * half + tt, :].bitcast(F32)
                         for u in range(2):
@@ -121,8 +105,9 @@ def tile_modulatedgraphconv_pa_t_e_kernel(tc, x, W_words, W_scales, M, adj, adj2
                                 words[:, 256 * g + u : 256 * (g + 1) : 2],
                                 ident[:],
                             )
+                    xg_words = xg[:, g, :].bitcast(F32).rearrange("p (n u) -> p n u", u=2)
                     nc.scalar.copy(
-                        out=xg_words[:, 2 * P * half : 2 * P * (half + 1), :],
+                        out=xg_words[:, HALF * half : HALF * (half + 1), :],
                         in_=xt[:].rearrange("p u n -> p n u"),
                     )
             return xg
@@ -130,10 +115,14 @@ def tile_modulatedgraphconv_pa_t_e_kernel(tc, x, W_words, W_scales, M, adj, adj2
         def quantise_x(xg):
             x_codes = xq_pool.tile([P, X_PASSES, NODES], U32, name="x_codes", align_bytes=64)
             x_scales = xq_pool.tile([P, X_PASSES, NODES], U8, name="x_scales", align_bytes=64)
-            for g in range(X_PASSES):
-                nc.vector.quantize_mx(
-                    out=x_codes[:, g, :].bitcast(FP8X4), scales=x_scales[:, g, :], in_=xg[:, g, :]
-                )
+            for half in range(2):
+                nodes = slice(HALF * half, HALF * (half + 1))
+                for g in range(X_PASSES):
+                    nc.vector.quantize_mx(
+                        out=x_codes[:, g, nodes].bitcast(FP8X4),
+                        scales=x_scales[:, g, nodes],
+                        in_=xg[:, g, PACK * HALF * half : PACK * HALF * (half + 1)],
+                    )
             return x_codes, x_scales
 
         def project(acc, xq, t, which, c0, width):
@@ -160,7 +149,7 @@ def tile_modulatedgraphconv_pa_t_e_kernel(tc, x, W_words, W_scales, M, adj, adj2
                 nc.gpsimd.tensor_tensor(out=o_sb[:, t, :], in0=o_sb[:, t, :], in1=bias_f32[:], op=ADD)
             return o_sb
 
-        def neighbour_operand(xq):
+        def neighbour_values(xq):
             g1 = g_pool.tile([P, COUT, PACK], BF16, name="g1", align_bytes=64)
             for s in range(COUT // P):
                 cols = slice(P * s, P * (s + 1))
@@ -170,6 +159,9 @@ def tile_modulatedgraphconv_pa_t_e_kernel(tc, x, W_words, W_scales, M, adj, adj2
                 nc.vector.tensor_tensor(
                     out=g1[:, cols, :], in0=h1[:].rearrange("p t c -> p c t"), in1=m_grouped[:, cols, :], op=MULT
                 )
+            return g1
+
+        def quantise_neighbours(g1):
             g_codes = g_pool.tile([P, COUT], U32, name="g_codes", align_bytes=64)
             g_scales = g_pool.tile([P, COUT], U8, name="g_scales", align_bytes=64)
             nc.vector.quantize_mx(
@@ -196,22 +188,63 @@ def tile_modulatedgraphconv_pa_t_e_kernel(tc, x, W_words, W_scales, M, adj, adj2
                 if t % 2 == 1:
                     nc.sync.dma_start(out=out_b[:, t - 1 : t + 1, :], in_=o_sb[:, t - 1 : t + 1, :])
 
+        bias_f32 = const.tile([P, COUT], F32)
+        nc.scalar.copy(out=bias_f32[:], in_=bias_bf[:])
+        a_self = const.tile([P, TILES], F32)
+        nc.vector.tensor_tensor(out=a_self[:], in0=diag_adj[:], in1=diag_adj2[:], op=ADD)
+
         xq = {0: quantise_x(transpose_x(0))}
+        ms = const.tile([P, TILES, COUT], F32)
         for t in range(TILES):
             nc.scalar.activation(out=ms[:, t, :], in_=m_sb[:, t, :], func=COPY, scale=a_self[:, t : t + 1])
-        nc.scalar.copy(out=bias_f32[:], in_=bias_bf[:])
-        nc.scalar.copy(out=m_grouped[:], in_=m_sb[:].rearrange("p t c -> p c t"))
+        m_grouped = const.tile([P, COUT, PACK], BF16)
+        nc.vector.tensor_copy(out=m_grouped[:], in_=m_sb[:].rearrange("p t c -> p c t"))
+        o_tiles = {0: self_term(xq[0])}
+        g1 = neighbour_values(xq[0])
+
+        adj2_half = const.tile([P, TILES, NODES], BF16)
+        nc.scalar.mul(out=adj2_half[:], in_=adj2_sb[:], mul=0.5)
+        s_half = const.tile([P, TILES * TILES, P], F32)
+        for t in range(TILES):
+            nc.vector.scalar_tensor_tensor(
+                out=s_half[:, TILES * t : TILES * (t + 1), :],
+                in0=adj_sb[:, t, :].rearrange("p (m t2) -> p t2 m", t2=TILES),
+                scalar=0.5,
+                in1=adj2_half[:, t, :].rearrange("p (m t2) -> p t2 m", t2=TILES),
+                op0=MULT,
+                op1=ADD,
+            )
+        diag_blocks = s_half[:, 0 : TILES * TILES : TILES + 1, :]
+        nc.vector.tensor_tensor(
+            out=diag_blocks, in0=diag_blocks, in1=off_diagonal[:].unsqueeze(1).to_broadcast([P, TILES, P]), op=MULT
+        )
+        gq = {0: quantise_neighbours(g1)}
+        for b in range(1, AHEAD + 1):
+            xq[b] = quantise_x(transpose_x(b))
+        a_grouped = const.tile([P, NODES, PACK], BF16, align_bytes=64)
+        for t2 in range(TILES):
+            flipped = psum_acc.tile([P, TILES, P], F32, name="flipped", tag="acc")
+            for t in range(TILES):
+                nc.tensor.transpose(flipped[:, t, :], s_half[:, TILES * t2 + t, :], ident[:])
+            nc.vector.tensor_tensor(
+                out=a_grouped[:, P * t2 : P * (t2 + 1), :],
+                in0=flipped[:].rearrange("p t m -> p m t"),
+                in1=s_half[:, t2 : TILES * TILES : TILES, :].rearrange("p t m -> p m t"),
+                op=ADD,
+            )
+        a_codes = const.tile([P, NODES], U32, align_bytes=64)
+        a_scales = const.tile([P, NODES], U8, align_bytes=64)
         nc.vector.quantize_mx(
             out=a_codes[:].bitcast(FP8X4), scales=a_scales[:], in_=a_grouped[:].rearrange("p w t -> p (w t)")
         )
-        gq = {}
-        o_tiles = {}
-        for b in range(BATCH + 1):
-            if b < BATCH:
-                o_tiles[b] = self_term(xq[b])
-            if b >= 1:
-                aggregate_and_store(b - 1, gq[b - 1], o_tiles[b - 1])
-            if b + 1 < BATCH:
-                xq[b + 1] = quantise_x(transpose_x(b + 1))
-            if b < BATCH:
-                gq[b] = neighbour_operand(xq[b])
+
+        for b in range(1, BATCH):
+            o_tiles[b] = self_term(xq[b])
+            if b + AHEAD < BATCH:
+                xg = transpose_x(b + AHEAD)
+            aggregate_and_store(b - 1, gq[b - 1], o_tiles[b - 1])
+            g1 = neighbour_values(xq[b])
+            if b + AHEAD < BATCH:
+                xq[b + AHEAD] = quantise_x(xg)
+            gq[b] = quantise_neighbours(g1)
+        aggregate_and_store(BATCH - 1, gq[BATCH - 1], o_tiles[BATCH - 1])

@@ -33,6 +33,7 @@ def tile_modulatedgraphconv_pa_t_e_kernel(tc, x, W_words, W_scales, M, adj, adj2
     with ExitStack() as ctx:
         const = ctx.enter_context(tc.tile_pool(name="const", bufs=1))
         x_pool = ctx.enter_context(tc.tile_pool(name="x_pool", bufs=BATCH))
+        xs_pool = ctx.enter_context(tc.tile_pool(name="xs_pool", bufs=2))
         xg_pool = ctx.enter_context(tc.tile_pool(name="xg_pool", bufs=2))
         xq_pool = ctx.enter_context(tc.tile_pool(name="xq_pool", bufs=AHEAD + 1))
         g_pool = ctx.enter_context(tc.tile_pool(name="g_pool", bufs=2))
@@ -92,25 +93,43 @@ def tile_modulatedgraphconv_pa_t_e_kernel(tc, x, W_words, W_scales, M, adj, adj2
             out=off_diagonal[:], in0=ident[:], scalar1=-1.0, scalar2=1.0, op0=MULT, op1=ADD
         )
 
-        def transpose_x(b):
-            xg = xg_pool.tile([P, X_PASSES, PACK * NODES], BF16, name="xg", align_bytes=64)
+        def sort_words(b):
+            x_sorted = xs_pool.tile([P, TILES, CIN // 2], F32, name="x_sorted")
             for half in range(2):
-                for g in range(X_PASSES):
-                    xt = psum_xt.tile([P, 2, HALF], F32, name="xt")
-                    for tt in range(2):
-                        words = x_sb[b][:, 2 * half + tt, :].bitcast(F32)
-                        for u in range(2):
-                            nc.tensor.transpose(
-                                xt[:, u, P * tt : P * (tt + 1)],
-                                words[:, 256 * g + u : 256 * (g + 1) : 2],
-                                ident[:],
-                            )
-                    xg_words = xg[:, g, :].bitcast(F32).rearrange("p (n u) -> p n u", u=2)
-                    nc.scalar.copy(
-                        out=xg_words[:, HALF * half : HALF * (half + 1), :],
-                        in_=xt[:].rearrange("p u n -> p n u"),
-                    )
-            return xg
+                tiles = slice(2 * half, 2 * half + 2)
+                nc.scalar.copy(
+                    out=x_sorted[:, tiles, :].rearrange("p t (g u q) -> p (t g) u q", u=2, q=P),
+                    in_=x_sb[b][:, tiles, :].bitcast(F32).rearrange("p t (g q u) -> p (t g) u q", u=2, q=P),
+                )
+            return x_sorted
+
+        def words_of(b, t, g, u):
+            if b in x_sorted:
+                return x_sorted[b][:, t, P * (2 * g + u) : P * (2 * g + u + 1)]
+            return x_sb[b][:, t, :].bitcast(F32)[:, 2 * P * g + u : 2 * P * (g + 1) : 2]
+
+        def transpose_x(b, xg, half):
+            for g in range(X_PASSES):
+                xt = psum_xt.tile([P, 2, HALF], F32, name="xt")
+                for tt in range(2):
+                    for u in range(2):
+                        nc.tensor.transpose(
+                            xt[:, u, P * tt : P * (tt + 1)], words_of(b, 2 * half + tt, g, u), ident[:]
+                        )
+                xg_words = xg[:, g, :].bitcast(F32).rearrange("p (n u) -> p n u", u=2)
+                nc.scalar.copy(
+                    out=xg_words[:, HALF * half : HALF * (half + 1), :],
+                    in_=xt[:].rearrange("p u n -> p n u"),
+                )
+
+        def new_xg():
+            return xg_pool.tile([P, X_PASSES, PACK * NODES], BF16, name="xg", align_bytes=64)
+
+        def prepare_x(b):
+            xg = new_xg()
+            transpose_x(b, xg, 0)
+            transpose_x(b, xg, 1)
+            return quantise_x(xg)
 
         def quantise_x(xg):
             x_codes = xq_pool.tile([P, X_PASSES, NODES], U32, name="x_codes", align_bytes=64)
@@ -193,7 +212,8 @@ def tile_modulatedgraphconv_pa_t_e_kernel(tc, x, W_words, W_scales, M, adj, adj2
         a_self = const.tile([P, TILES], F32)
         nc.vector.tensor_tensor(out=a_self[:], in0=diag_adj[:], in1=diag_adj2[:], op=ADD)
 
-        xq = {0: quantise_x(transpose_x(0))}
+        x_sorted = {}
+        xq = {0: prepare_x(0)}
         ms = const.tile([P, TILES, COUT], F32)
         for t in range(TILES):
             nc.scalar.activation(out=ms[:, t, :], in_=m_sb[:, t, :], func=COPY, scale=a_self[:, t : t + 1])
@@ -220,7 +240,8 @@ def tile_modulatedgraphconv_pa_t_e_kernel(tc, x, W_words, W_scales, M, adj, adj2
         )
         gq = {0: quantise_neighbours(g1)}
         for b in range(1, AHEAD + 1):
-            xq[b] = quantise_x(transpose_x(b))
+            xq[b] = prepare_x(b)
+        x_sorted[AHEAD + 1] = sort_words(AHEAD + 1)
         a_grouped = const.tile([P, NODES, PACK], BF16, align_bytes=64)
         for t2 in range(TILES):
             flipped = psum_acc.tile([P, TILES, P], F32, name="flipped", tag="acc")
@@ -239,12 +260,18 @@ def tile_modulatedgraphconv_pa_t_e_kernel(tc, x, W_words, W_scales, M, adj, adj2
         )
 
         for b in range(1, BATCH):
+            ahead = b + AHEAD
+            if ahead < BATCH:
+                xg = new_xg()
+                transpose_x(ahead, xg, 0)
             o_tiles[b] = self_term(xq[b])
-            if b + AHEAD < BATCH:
-                xg = transpose_x(b + AHEAD)
+            if ahead < BATCH:
+                transpose_x(ahead, xg, 1)
             aggregate_and_store(b - 1, gq[b - 1], o_tiles[b - 1])
             g1 = neighbour_values(xq[b])
-            if b + AHEAD < BATCH:
-                xq[b + AHEAD] = quantise_x(xg)
+            if ahead < BATCH:
+                xq[ahead] = quantise_x(xg)
             gq[b] = quantise_neighbours(g1)
+            if ahead + 1 < BATCH:
+                x_sorted[ahead + 1] = sort_words(ahead + 1)
         aggregate_and_store(BATCH - 1, gq[BATCH - 1], o_tiles[BATCH - 1])

@@ -164,7 +164,11 @@ def tile_modulatedgraphconv_pa_t_e_kernel(tc, x, W_words, W_scales, M, adj, adj2
             for t in range(TILES):
                 h0 = psum_acc.tile([P, COUT], F32, name="h0", tag="acc")
                 project(h0[:], xq, t, 0, 0, COUT)
-                nc.vector.tensor_tensor(out=o_sb[:, t, :], in0=h0[:], in1=ms[:, t, :], op=MULT)
+                if t == 0:
+                    nc.scalar.activation(out=o_sb[:, t, :], in_=h0[:], func=COPY, scale=a_self[:, t : t + 1])
+                    nc.gpsimd.tensor_tensor(out=o_sb[:, t, :], in0=o_sb[:, t, :], in1=m_sb[:, t, :], op=MULT)
+                else:
+                    nc.vector.tensor_tensor(out=o_sb[:, t, :], in0=h0[:], in1=ms[:, t, :], op=MULT)
                 nc.gpsimd.tensor_tensor(out=o_sb[:, t, :], in0=o_sb[:, t, :], in1=bias_f32[:], op=ADD)
             return o_sb
 
@@ -204,8 +208,7 @@ def tile_modulatedgraphconv_pa_t_e_kernel(tc, x, W_words, W_scales, M, adj, adj2
                     stop=True,
                 )
                 nc.vector.tensor_tensor(out=o_sb[:, t, :], in0=agg[:], in1=o_sb[:, t, :], op=ADD)
-                if t % 2 == 1:
-                    nc.sync.dma_start(out=out_b[:, t - 1 : t + 1, :], in_=o_sb[:, t - 1 : t + 1, :])
+                nc.sync.dma_start(out=out_b[:, t, :], in_=o_sb[:, t, :])
 
         bias_f32 = const.tile([P, COUT], F32)
         nc.scalar.copy(out=bias_f32[:], in_=bias_bf[:])
@@ -215,7 +218,7 @@ def tile_modulatedgraphconv_pa_t_e_kernel(tc, x, W_words, W_scales, M, adj, adj2
         x_sorted = {}
         xq = {0: prepare_x(0)}
         ms = const.tile([P, TILES, COUT], F32)
-        for t in range(TILES):
+        for t in range(1, TILES):
             nc.scalar.activation(out=ms[:, t, :], in_=m_sb[:, t, :], func=COPY, scale=a_self[:, t : t + 1])
         m_grouped = const.tile([P, COUT, PACK], BF16)
         nc.vector.tensor_copy(out=m_grouped[:], in_=m_sb[:].rearrange("p t c -> p c t"))
@@ -259,7 +262,7 @@ def tile_modulatedgraphconv_pa_t_e_kernel(tc, x, W_words, W_scales, M, adj, adj2
             out=a_codes[:].bitcast(FP8X4), scales=a_scales[:], in_=a_grouped[:].rearrange("p w t -> p (w t)")
         )
 
-        for b in range(1, BATCH):
+        for b in range(1, BATCH - 1):
             ahead = b + AHEAD
             if ahead < BATCH:
                 xg = new_xg()
@@ -274,4 +277,8 @@ def tile_modulatedgraphconv_pa_t_e_kernel(tc, x, W_words, W_scales, M, adj, adj2
             gq[b] = quantise_neighbours(g1)
             if ahead + 1 < BATCH:
                 x_sorted[ahead + 1] = sort_words(ahead + 1)
-        aggregate_and_store(BATCH - 1, gq[BATCH - 1], o_tiles[BATCH - 1])
+        last = BATCH - 1
+        gq[last] = quantise_neighbours(neighbour_values(xq[last]))
+        o_tiles[last] = self_term(xq[last])
+        aggregate_and_store(last - 1, gq[last - 1], o_tiles[last - 1])
+        aggregate_and_store(last, gq[last], o_tiles[last])

@@ -129,9 +129,19 @@ def tile_modulatedgraphconv_pa_t_e_kernel(tc, x, W_words, W_scales, M, adj, adj2
             xg = new_xg()
             transpose_x(b, xg, 0)
             transpose_x(b, xg, 1)
-            return quantise_x(xg)
+            return quantise_first_x(xg) if b == 0 else quantise_x(xg)
 
         def quantise_x(xg):
+            x_codes = xq_pool.tile([P, X_PASSES, NODES], U32, name="x_codes", align_bytes=64)
+            x_scales = xq_pool.tile([P, X_PASSES, NODES], U8, name="x_scales", align_bytes=64)
+            nc.vector.quantize_mx(
+                out=x_codes[:].rearrange("p g n -> p (g n)").bitcast(FP8X4),
+                scales=x_scales[:].rearrange("p g n -> p (g n)"),
+                in_=xg[:].rearrange("p g w -> p (g w)"),
+            )
+            return x_codes, x_scales
+
+        def quantise_first_x(xg):
             x_codes = xq_pool.tile([P, X_PASSES, NODES], U32, name="x_codes", align_bytes=64)
             x_scales = xq_pool.tile([P, X_PASSES, NODES], U8, name="x_scales", align_bytes=64)
             for half in range(2):

@@ -42,26 +42,15 @@ def tile_modulatedgraphconv_pa_t_e_kernel(tc, x, W_words, W_scales, M, adj, adj2
         psum_acc = ctx.enter_context(tc.psum_pool(name="psum_acc", bufs=5))
         ctx.enter_context(tc.manual_schedule())
 
-        diag_adj = const.tile([P, TILES], BF16)
-        diag_adj2 = const.tile([P, TILES], BF16)
-        with nc.allow_non_contiguous_dma(reason="the 512 diagonal elements of a matrix"):
-            for diag_sb, matrix in ((diag_adj, adj), (diag_adj2, adj2)):
-                nc.scalar.dma_start(
-                    out=diag_sb[:],
-                    in_=matrix.rearrange("i j -> (i j)")[0 : NODES * NODES : NODES + 1].rearrange(
-                        "(p t) -> p t", t=TILES
-                    ),
-                )
-        bias_bf = const.tile([P, COUT], BF16)
-        nc.gpsimd.dma_start(out=bias_bf[:], in_=bias.partition_broadcast(P))
+        bias_row = const.tile([P, COUT], BF16)
+        nc.vector.memset(bias_row[:], 0.0)
+        first_row = const.tile([P, P], BF16)
+        nc.vector.memset(first_row[:], 0.0)
+        nc.vector.memset(first_row[0:1, :], 1.0)
+        nc.scalar.dma_start(out=bias_row[0:1, :], in_=bias.unsqueeze(0))
 
-        w_scales = const.tile([P, 2 * X_PASSES, COUT], U8, align_bytes=64)
+        w_scales = const.tile([P, COUT], U8, align_bytes=64)
         nc.vector.memset(w_scales[:].bitcast(I32), 0)
-        for quadrant in range(4):
-            nc.sync.dma_start(
-                out=w_scales[:].bitcast(I32)[32 * quadrant : 32 * quadrant + 4, :, :],
-                in_=W_scales.bitcast(I32)[:, 4 * quadrant : 4 * quadrant + 4, :].rearrange("g r n -> r g n"),
-            )
         x_sb = [x_pool.tile([P, TILES, CIN], BF16, name="x_sb") for b in range(BATCH)]
 
         def load_x(b):
@@ -71,19 +60,31 @@ def tile_modulatedgraphconv_pa_t_e_kernel(tc, x, W_words, W_scales, M, adj, adj2
                 nc.sync.dma_start(out=x_sb[b][:, tiles, :], in_=x_b[:, tiles, :])
 
         load_x(0)
-        m_sb = const.tile([P, TILES, COUT], BF16)
-        nc.sync.dma_start(out=m_sb[:], in_=M.rearrange("(p t) c -> p t c", t=TILES))
+        for quadrant in range(4):
+            nc.sync.dma_start(
+                out=w_scales[:].bitcast(I32)[32 * quadrant : 32 * quadrant + 4 * 2 * X_PASSES, :],
+                in_=W_scales.bitcast(I32)[:, 4 * quadrant : 4 * quadrant + 4, :],
+            )
         w_words = const.tile([P, 2 * X_PASSES, PACK * COUT], U8, align_bytes=64)
-        for g in range(2 * X_PASSES):
+
+        def load_w(g):
             nc.sync.dma_start(
                 out=w_words[:, g, :].bitcast(I32),
                 in_=W_words[g].rearrange("p n t -> p (n t)").bitcast(I32),
             )
+
+        load_w(0)
+        load_w(1)
+        m_sb = const.tile([P, TILES, COUT], BF16)
+        nc.sync.dma_start(out=m_sb[:], in_=M.rearrange("(p t) c -> p t c", t=TILES))
+        load_w(2)
+        load_w(3)
+        load_x(1)
         adj_sb = const.tile([P, TILES, NODES], BF16)
         adj2_sb = const.tile([P, TILES, NODES], BF16)
         nc.sync.dma_start(out=adj2_sb[:], in_=adj2.rearrange("(p t) i -> p t i", t=TILES))
         nc.sync.dma_start(out=adj_sb[:], in_=adj.rearrange("(p t) i -> p t i", t=TILES))
-        for b in range(1, BATCH):
+        for b in range(2, BATCH):
             load_x(b)
 
         ident = const.tile([P, P], F32)
@@ -129,7 +130,7 @@ def tile_modulatedgraphconv_pa_t_e_kernel(tc, x, W_words, W_scales, M, adj, adj2
             xg = new_xg()
             transpose_x(b, xg, 0)
             transpose_x(b, xg, 1)
-            return quantise_first_x(xg) if b == 0 else quantise_x(xg)
+            return quantise_x(xg)
 
         def quantise_x(xg):
             x_codes = xq_pool.tile([P, X_PASSES, NODES], U32, name="x_codes", align_bytes=64)
@@ -164,7 +165,7 @@ def tile_modulatedgraphconv_pa_t_e_kernel(tc, x, W_words, W_scales, M, adj, adj2
                     lhsT=x_codes[:, g, nodes].bitcast(FP8X4),
                     lhsT_scale=x_scales[:, g, nodes],
                     rhs=w_words[:, wg, PACK * c0 : PACK * (c0 + width)].bitcast(FP8X4),
-                    rhs_scale=w_scales[:, wg, c0 : c0 + width],
+                    rhs_scale=w_scales[4 * wg : P, c0 : c0 + width],
                     start=(g == 0),
                     stop=(g == X_PASSES - 1),
                 )
@@ -221,12 +222,27 @@ def tile_modulatedgraphconv_pa_t_e_kernel(tc, x, W_words, W_scales, M, adj, adj2
                 nc.sync.dma_start(out=out_b[:, t, :], in_=o_sb[:, t, :])
 
         bias_f32 = const.tile([P, COUT], F32)
-        nc.scalar.copy(out=bias_f32[:], in_=bias_bf[:])
-        a_self = const.tile([P, TILES], F32)
-        nc.vector.tensor_tensor(out=a_self[:], in0=diag_adj[:], in1=diag_adj2[:], op=ADD)
+        spread = psum_acc.tile([P, COUT], F32, name="spread", tag="acc")
+        nc.tensor.matmul(spread[:], lhsT=first_row[:], rhs=bias_row[:], start=True, stop=True)
+        nc.scalar.copy(out=bias_f32[:], in_=spread[:])
 
         x_sorted = {}
-        xq = {0: prepare_x(0)}
+        xg = new_xg()
+        transpose_x(0, xg, 0)
+        diag_adj = const.tile([P, TILES], BF16)
+        diag_adj2 = const.tile([P, TILES], BF16)
+        with nc.allow_non_contiguous_dma(reason="the 512 diagonal elements of a matrix"):
+            for diag_sb, matrix in ((diag_adj, adj), (diag_adj2, adj2)):
+                nc.scalar.dma_start(
+                    out=diag_sb[:],
+                    in_=matrix.rearrange("i j -> (i j)")[0 : NODES * NODES : NODES + 1].rearrange(
+                        "(p t) -> p t", t=TILES
+                    ),
+                )
+        transpose_x(0, xg, 1)
+        xq = {0: quantise_first_x(xg)}
+        a_self = const.tile([P, TILES], F32)
+        nc.vector.tensor_tensor(out=a_self[:], in0=diag_adj[:], in1=diag_adj2[:], op=ADD)
         ms = const.tile([P, TILES, COUT], F32)
         for t in range(1, TILES):
             nc.scalar.activation(out=ms[:, t, :], in_=m_sb[:, t, :], func=COPY, scale=a_self[:, t : t + 1])

@@ -42,6 +42,16 @@ def tile_modulatedgraphconv_pa_t_e_kernel(tc, x, W_words, W_scales, M, adj, adj2
         psum_acc = ctx.enter_context(tc.psum_pool(name="psum_acc", bufs=5))
         ctx.enter_context(tc.manual_schedule())
 
+        diag_adj = const.tile([P, TILES], BF16)
+        diag_adj2 = const.tile([P, TILES], BF16)
+        with nc.allow_non_contiguous_dma(reason="the 512 diagonal elements of a matrix"):
+            for diag_sb, matrix in ((diag_adj, adj), (diag_adj2, adj2)):
+                nc.scalar.dma_start(
+                    out=diag_sb[:],
+                    in_=matrix.rearrange("i j -> (i j)")[0 : NODES * NODES : NODES + 1].rearrange(
+                        "(p t) -> p t", t=TILES
+                    ),
+                )
         bias_row = const.tile([P, COUT], BF16)
         nc.vector.memset(bias_row[:], 0.0)
         first_row = const.tile([P, P], BF16)
@@ -109,27 +119,25 @@ def tile_modulatedgraphconv_pa_t_e_kernel(tc, x, W_words, W_scales, M, adj, adj2
                 return x_sorted[b][:, t, P * (2 * g + u) : P * (2 * g + u + 1)]
             return x_sb[b][:, t, :].bitcast(F32)[:, 2 * P * g + u : 2 * P * (g + 1) : 2]
 
-        def transpose_x(b, xg, half):
-            for g in range(X_PASSES):
-                xt = psum_xt.tile([P, 2, HALF], F32, name="xt")
-                for tt in range(2):
-                    for u in range(2):
-                        nc.tensor.transpose(
-                            xt[:, u, P * tt : P * (tt + 1)], words_of(b, 2 * half + tt, g, u), ident[:]
-                        )
-                xg_words = xg[:, g, :].bitcast(F32).rearrange("p (n u) -> p n u", u=2)
-                nc.scalar.copy(
-                    out=xg_words[:, HALF * half : HALF * (half + 1), :],
-                    in_=xt[:].rearrange("p u n -> p n u"),
-                )
+        def transpose_x(b, xg, part):
+            half, g = divmod(part, X_PASSES)
+            xt = psum_xt.tile([P, 2, HALF], F32, name="xt")
+            for tt in range(2):
+                for u in range(2):
+                    nc.tensor.transpose(xt[:, u, P * tt : P * (tt + 1)], words_of(b, 2 * half + tt, g, u), ident[:])
+            xg_words = xg[:, g, :].bitcast(F32).rearrange("p (n u) -> p n u", u=2)
+            nc.scalar.copy(
+                out=xg_words[:, HALF * half : HALF * (half + 1), :],
+                in_=xt[:].rearrange("p u n -> p n u"),
+            )
 
         def new_xg():
             return xg_pool.tile([P, X_PASSES, PACK * NODES], BF16, name="xg", align_bytes=64)
 
         def prepare_x(b):
             xg = new_xg()
-            transpose_x(b, xg, 0)
-            transpose_x(b, xg, 1)
+            for part in range(4):
+                transpose_x(b, xg, part)
             return quantise_x(xg)
 
         def quantise_x(xg):
@@ -228,18 +236,8 @@ def tile_modulatedgraphconv_pa_t_e_kernel(tc, x, W_words, W_scales, M, adj, adj2
 
         x_sorted = {}
         xg = new_xg()
-        transpose_x(0, xg, 0)
-        diag_adj = const.tile([P, TILES], BF16)
-        diag_adj2 = const.tile([P, TILES], BF16)
-        with nc.allow_non_contiguous_dma(reason="the 512 diagonal elements of a matrix"):
-            for diag_sb, matrix in ((diag_adj, adj), (diag_adj2, adj2)):
-                nc.scalar.dma_start(
-                    out=diag_sb[:],
-                    in_=matrix.rearrange("i j -> (i j)")[0 : NODES * NODES : NODES + 1].rearrange(
-                        "(p t) -> p t", t=TILES
-                    ),
-                )
-        transpose_x(0, xg, 1)
+        for part in range(4):
+            transpose_x(0, xg, part)
         xq = {0: quantise_first_x(xg)}
         a_self = const.tile([P, TILES], F32)
         nc.vector.tensor_tensor(out=a_self[:], in0=diag_adj[:], in1=diag_adj2[:], op=ADD)
@@ -292,10 +290,9 @@ def tile_modulatedgraphconv_pa_t_e_kernel(tc, x, W_words, W_scales, M, adj, adj2
             ahead = b + AHEAD
             if ahead < BATCH:
                 xg = new_xg()
-                transpose_x(ahead, xg, 0)
+                for part in range(4):
+                    transpose_x(ahead, xg, part)
             o_tiles[b] = self_term(xq[b])
-            if ahead < BATCH:
-                transpose_x(ahead, xg, 1)
             aggregate_and_store(b - 1, gq[b - 1], o_tiles[b - 1])
             g1 = neighbour_values(xq[b])
             if ahead < BATCH:

@@ -183,11 +183,7 @@ def tile_modulatedgraphconv_pa_t_e_kernel(tc, x, W_words, W_scales, M, adj, adj2
             for t in range(TILES):
                 h0 = psum_acc.tile([P, COUT], F32, name="h0", tag="acc")
                 project(h0[:], xq, t, 0, 0, COUT)
-                if t == 0:
-                    nc.scalar.activation(out=o_sb[:, t, :], in_=h0[:], func=COPY, scale=a_self[:, t : t + 1])
-                    nc.gpsimd.tensor_tensor(out=o_sb[:, t, :], in0=o_sb[:, t, :], in1=m_sb[:, t, :], op=MULT)
-                else:
-                    nc.vector.tensor_tensor(out=o_sb[:, t, :], in0=h0[:], in1=ms[:, t, :], op=MULT)
+                nc.vector.tensor_tensor(out=o_sb[:, t, :], in0=h0[:], in1=ms[:, t, :], op=MULT)
                 nc.gpsimd.tensor_tensor(out=o_sb[:, t, :], in0=o_sb[:, t, :], in1=bias_f32[:], op=ADD)
             return o_sb
 
@@ -242,7 +238,7 @@ def tile_modulatedgraphconv_pa_t_e_kernel(tc, x, W_words, W_scales, M, adj, adj2
         a_self = const.tile([P, TILES], F32)
         nc.vector.tensor_tensor(out=a_self[:], in0=diag_adj[:], in1=diag_adj2[:], op=ADD)
         ms = const.tile([P, TILES, COUT], F32)
-        for t in range(1, TILES):
+        for t in range(TILES):
             nc.scalar.activation(out=ms[:, t, :], in_=m_sb[:, t, :], func=COPY, scale=a_self[:, t : t + 1])
         m_grouped = const.tile([P, COUT, PACK], BF16)
         nc.vector.tensor_copy(out=m_grouped[:], in_=m_sb[:].rearrange("p t c -> p c t"))

@@ -184,7 +184,11 @@ def tile_modulatedgraphconv_pa_t_e_kernel(tc, x, W_words, W_scales, M, adj, adj2
                 h0 = psum_acc.tile([P, COUT], F32, name="h0", tag="acc")
                 project(h0[:], xq, t, 0, 0, COUT)
                 nc.vector.tensor_tensor(out=o_sb[:, t, :], in0=h0[:], in1=ms[:, t, :], op=MULT)
-                nc.gpsimd.tensor_tensor(out=o_sb[:, t, :], in0=o_sb[:, t, :], in1=bias_f32[:], op=ADD)
+                if t % 2 == 1:
+                    pair = o_sb[:, t - 1 : t + 1, :]
+                    nc.gpsimd.tensor_tensor(
+                        out=pair, in0=pair, in1=bias_f32[:].unsqueeze(1).to_broadcast([P, 2, COUT]), op=ADD
+                    )
             return o_sb
 
         def neighbour_values(xq):
@@ -225,15 +229,15 @@ def tile_modulatedgraphconv_pa_t_e_kernel(tc, x, W_words, W_scales, M, adj, adj2
                 nc.vector.tensor_tensor(out=o_sb[:, t, :], in0=agg[:], in1=o_sb[:, t, :], op=ADD)
                 nc.sync.dma_start(out=out_b[:, t, :], in_=o_sb[:, t, :])
 
+        x_sorted = {}
+        xg = new_xg()
+        for part in range(4):
+            transpose_x(0, xg, part)
         bias_f32 = const.tile([P, COUT], F32)
         spread = psum_acc.tile([P, COUT], F32, name="spread", tag="acc")
         nc.tensor.matmul(spread[:], lhsT=first_row[:], rhs=bias_row[:], start=True, stop=True)
         nc.scalar.copy(out=bias_f32[:], in_=spread[:])
 
-        x_sorted = {}
-        xg = new_xg()
-        for part in range(4):
-            transpose_x(0, xg, part)
         xq = {0: quantise_first_x(xg)}
         a_self = const.tile([P, TILES], F32)
         nc.vector.tensor_tensor(out=a_self[:], in0=diag_adj[:], in1=diag_adj2[:], op=ADD)

@@ -178,12 +178,22 @@ def tile_modulatedgraphconv_pa_t_e_kernel(tc, x, W_words, W_scales, M, adj, adj2
                     stop=(g == X_PASSES - 1),
                 )
 
-        def self_term(xq):
+        def self_term(b):
             o_sb = o_pool.tile([P, TILES, COUT], F32, name="o_sb")
             for t in range(TILES):
                 h0 = psum_acc.tile([P, COUT], F32, name="h0", tag="acc")
-                project(h0[:], xq, t, 0, 0, COUT)
-                nc.vector.tensor_tensor(out=o_sb[:, t, :], in0=h0[:], in1=ms[:, t, :], op=MULT)
+                project(h0[:], xq[b], t, 0, 0, COUT)
+                if b == 0:
+                    nc.vector.scalar_tensor_tensor(
+                        out=o_sb[:, t, :],
+                        in0=h0[:],
+                        scalar=a_self[:, t : t + 1],
+                        in1=m_sb[:, t, :],
+                        op0=MULT,
+                        op1=MULT,
+                    )
+                else:
+                    nc.vector.tensor_tensor(out=o_sb[:, t, :], in0=h0[:], in1=ms[:, t, :], op=MULT)
                 if t % 2 == 1:
                     pair = o_sb[:, t - 1 : t + 1, :]
                     nc.gpsimd.tensor_tensor(
@@ -211,10 +221,11 @@ def tile_modulatedgraphconv_pa_t_e_kernel(tc, x, W_words, W_scales, M, adj, adj2
             )
             return g_codes, g_scales
 
-        def aggregate_and_store(b, gq, o_sb):
-            g_codes, g_scales = gq
+        def aggregate_and_store(b, tiles=range(TILES)):
+            g_codes, g_scales = gq[b]
+            o_sb = o_tiles[b]
             out_b = out[b].rearrange("(p t) c -> p t c", t=TILES)
-            for t in range(TILES):
+            for t in tiles:
                 nodes = slice(P * t, P * (t + 1))
                 agg = psum_acc.tile([P, COUT], F32, name="agg", tag="acc")
                 nc.tensor.matmul_mx(
@@ -241,27 +252,24 @@ def tile_modulatedgraphconv_pa_t_e_kernel(tc, x, W_words, W_scales, M, adj, adj2
         xq = {0: quantise_first_x(xg)}
         a_self = const.tile([P, TILES], F32)
         nc.vector.tensor_tensor(out=a_self[:], in0=diag_adj[:], in1=diag_adj2[:], op=ADD)
+        m_grouped = const.tile([P, COUT, PACK], BF16)
+        for half in range(2):
+            cols = slice(COUT // 2 * half, COUT // 2 * (half + 1))
+            nc.scalar.mul(out=m_grouped[:, cols, :], in_=m_sb[:, :, cols].rearrange("p t c -> p c t"), mul=0.5)
         ms = const.tile([P, TILES, COUT], F32)
         for t in range(TILES):
             nc.scalar.activation(out=ms[:, t, :], in_=m_sb[:, t, :], func=COPY, scale=a_self[:, t : t + 1])
-        m_grouped = const.tile([P, COUT, PACK], BF16)
-        nc.vector.tensor_copy(out=m_grouped[:], in_=m_sb[:].rearrange("p t c -> p c t"))
-        o_tiles = {0: self_term(xq[0])}
+        o_tiles = {0: self_term(0)}
         g1 = neighbour_values(xq[0])
 
-        adj2_half = const.tile([P, TILES, NODES], BF16)
-        nc.scalar.mul(out=adj2_half[:], in_=adj2_sb[:], mul=0.5)
-        s_half = const.tile([P, TILES * TILES, P], F32)
-        for t in range(TILES):
-            nc.vector.scalar_tensor_tensor(
-                out=s_half[:, TILES * t : TILES * (t + 1), :],
-                in0=adj_sb[:, t, :].rearrange("p (m t2) -> p t2 m", t2=TILES),
-                scalar=0.5,
-                in1=adj2_half[:, t, :].rearrange("p (m t2) -> p t2 m", t2=TILES),
-                op0=MULT,
-                op1=ADD,
-            )
-        diag_blocks = s_half[:, 0 : TILES * TILES : TILES + 1, :]
+        s = const.tile([P, TILES * TILES, P], F32)
+        nc.vector.tensor_tensor(
+            out=s[:].rearrange("p (t t2) m -> p t t2 m", t2=TILES),
+            in0=adj_sb[:].rearrange("p t (m t2) -> p t t2 m", t2=TILES),
+            in1=adj2_sb[:].rearrange("p t (m t2) -> p t t2 m", t2=TILES),
+            op=ADD,
+        )
+        diag_blocks = s[:, 0 : TILES * TILES : TILES + 1, :]
         nc.vector.tensor_tensor(
             out=diag_blocks, in0=diag_blocks, in1=off_diagonal[:].unsqueeze(1).to_broadcast([P, TILES, P]), op=MULT
         )
@@ -273,11 +281,11 @@ def tile_modulatedgraphconv_pa_t_e_kernel(tc, x, W_words, W_scales, M, adj, adj2
         for t2 in range(TILES):
             flipped = psum_acc.tile([P, TILES, P], F32, name="flipped", tag="acc")
             for t in range(TILES):
-                nc.tensor.transpose(flipped[:, t, :], s_half[:, TILES * t2 + t, :], ident[:])
+                nc.tensor.transpose(flipped[:, t, :], s[:, TILES * t2 + t, :], ident[:])
             nc.vector.tensor_tensor(
                 out=a_grouped[:, P * t2 : P * (t2 + 1), :],
                 in0=flipped[:].rearrange("p t m -> p m t"),
-                in1=s_half[:, t2 : TILES * TILES : TILES, :].rearrange("p t m -> p m t"),
+                in1=s[:, t2 : TILES * TILES : TILES, :].rearrange("p t m -> p m t"),
                 op=ADD,
             )
         a_codes = const.tile([P, NODES], U32, align_bytes=64)
@@ -292,8 +300,8 @@ def tile_modulatedgraphconv_pa_t_e_kernel(tc, x, W_words, W_scales, M, adj, adj2
                 xg = new_xg()
                 for part in range(4):
                     transpose_x(ahead, xg, part)
-            o_tiles[b] = self_term(xq[b])
-            aggregate_and_store(b - 1, gq[b - 1], o_tiles[b - 1])
+            o_tiles[b] = self_term(b)
+            aggregate_and_store(b - 1)
             g1 = neighbour_values(xq[b])
             if ahead < BATCH:
                 xq[ahead] = quantise_x(xg)
@@ -301,7 +309,10 @@ def tile_modulatedgraphconv_pa_t_e_kernel(tc, x, W_words, W_scales, M, adj, adj2
             if ahead + 1 < BATCH:
                 x_sorted[ahead + 1] = sort_words(ahead + 1)
         last = BATCH - 1
-        gq[last] = quantise_neighbours(neighbour_values(xq[last]))
-        o_tiles[last] = self_term(xq[last])
-        aggregate_and_store(last - 1, gq[last - 1], o_tiles[last - 1])
-        aggregate_and_store(last, gq[last], o_tiles[last])
+        o_tiles[last] = self_term(last)
+        aggregate_and_store(last - 1, range(2))
+        g1 = neighbour_values(xq[last])
+        aggregate_and_store(last - 1, range(2, 3))
+        gq[last] = quantise_neighbours(g1)
+        aggregate_and_store(last - 1, range(3, TILES))
+        aggregate_and_store(last)

@@ -32,12 +32,12 @@ def tile_modulatedgraphconv_pa_t_e_kernel(tc, x, W_words, W_scales, M, adj, adj2
     nc = tc.nc
     with ExitStack() as ctx:
         const = ctx.enter_context(tc.tile_pool(name="const", bufs=1))
-        x_pool = ctx.enter_context(tc.tile_pool(name="x_pool", bufs=BATCH))
+        x_pool = ctx.enter_context(tc.tile_pool(name="x_pool", bufs=BATCH - 2))
         xs_pool = ctx.enter_context(tc.tile_pool(name="xs_pool", bufs=2))
         xg_pool = ctx.enter_context(tc.tile_pool(name="xg_pool", bufs=2))
         xq_pool = ctx.enter_context(tc.tile_pool(name="xq_pool", bufs=AHEAD + 1))
         g_pool = ctx.enter_context(tc.tile_pool(name="g_pool", bufs=2))
-        o_pool = ctx.enter_context(tc.tile_pool(name="o_pool", bufs=3))
+        o_pool = ctx.enter_context(tc.tile_pool(name="o_pool", bufs=BATCH))
         psum_xt = ctx.enter_context(tc.psum_pool(name="psum_xt", bufs=3))
         psum_acc = ctx.enter_context(tc.psum_pool(name="psum_acc", bufs=5))
         ctx.enter_context(tc.manual_schedule())
@@ -61,9 +61,10 @@ def tile_modulatedgraphconv_pa_t_e_kernel(tc, x, W_words, W_scales, M, adj, adj2
 
         w_scales = const.tile([P, COUT], U8, align_bytes=64)
         nc.vector.memset(w_scales[:].bitcast(I32), 0)
-        x_sb = [x_pool.tile([P, TILES, CIN], BF16, name="x_sb") for b in range(BATCH)]
+        x_sb = {}
 
         def load_x(b):
+            x_sb[b] = x_pool.tile([P, TILES, CIN], BF16, name="x_sb_b")
             x_b = x[b].rearrange("(p t) k -> p t k", t=TILES)
             for half in range(2):
                 tiles = slice(2 * half, 2 * half + 2)
@@ -94,7 +95,7 @@ def tile_modulatedgraphconv_pa_t_e_kernel(tc, x, W_words, W_scales, M, adj, adj2
         adj2_sb = const.tile([P, TILES, NODES], BF16)
         nc.sync.dma_start(out=adj2_sb[:], in_=adj2.rearrange("(p t) i -> p t i", t=TILES))
         nc.sync.dma_start(out=adj_sb[:], in_=adj.rearrange("(p t) i -> p t i", t=TILES))
-        for b in range(2, BATCH):
+        for b in range(2, BATCH - 2):
             load_x(b)
 
         ident = const.tile([P, P], F32)
@@ -197,7 +198,7 @@ def tile_modulatedgraphconv_pa_t_e_kernel(tc, x, W_words, W_scales, M, adj, adj2
                 if t % 2 == 1:
                     pair = o_sb[:, t - 1 : t + 1, :]
                     nc.gpsimd.tensor_tensor(
-                        out=pair, in0=pair, in1=bias_f32[:].unsqueeze(1).to_broadcast([P, 2, COUT]), op=ADD
+                        out=pair, in0=pair, in1=bias_all[:].unsqueeze(1).to_broadcast([P, 2, COUT]), op=ADD
                     )
             return o_sb
 
@@ -244,10 +245,10 @@ def tile_modulatedgraphconv_pa_t_e_kernel(tc, x, W_words, W_scales, M, adj, adj2
         xg = new_xg()
         for part in range(4):
             transpose_x(0, xg, part)
-        bias_f32 = const.tile([P, COUT], F32)
+        bias_all = const.tile([P, COUT], BF16)
         spread = psum_acc.tile([P, COUT], F32, name="spread", tag="acc")
         nc.tensor.matmul(spread[:], lhsT=first_row[:], rhs=bias_row[:], start=True, stop=True)
-        nc.scalar.copy(out=bias_f32[:], in_=spread[:])
+        nc.scalar.copy(out=bias_all[:], in_=spread[:])
 
         xq = {0: quantise_first_x(xg)}
         a_self = const.tile([P, TILES], F32)
@@ -277,6 +278,8 @@ def tile_modulatedgraphconv_pa_t_e_kernel(tc, x, W_words, W_scales, M, adj, adj2
         for b in range(1, AHEAD + 1):
             xq[b] = prepare_x(b)
         x_sorted[AHEAD + 1] = sort_words(AHEAD + 1)
+        for b in range(BATCH - 2, BATCH):
+            load_x(b)
         a_grouped = const.tile([P, NODES, PACK], BF16, align_bytes=64)
         for t2 in range(TILES):
             flipped = psum_acc.tile([P, TILES, P], F32, name="flipped", tag="acc")

@@ -38,6 +38,7 @@ def tile_modulatedgraphconv_pa_t_e_kernel(tc, x, W_words, W_scales, M, adj, adj2
         xq_pool = ctx.enter_context(tc.tile_pool(name="xq_pool", bufs=AHEAD + 1))
         g_pool = ctx.enter_context(tc.tile_pool(name="g_pool", bufs=2))
         o_pool = ctx.enter_context(tc.tile_pool(name="o_pool", bufs=BATCH))
+        agg_pool = ctx.enter_context(tc.tile_pool(name="agg_pool", bufs=1))
         psum_xt = ctx.enter_context(tc.psum_pool(name="psum_xt", bufs=3))
         psum_acc = ctx.enter_context(tc.psum_pool(name="psum_acc", bufs=5))
         ctx.enter_context(tc.manual_schedule())
@@ -105,67 +106,72 @@ def tile_modulatedgraphconv_pa_t_e_kernel(tc, x, W_words, W_scales, M, adj, adj2
             out=off_diagonal[:], in0=ident[:], scalar1=-1.0, scalar2=1.0, op0=MULT, op1=ADD
         )
 
+        x_sorted = {}
+        xg_tiles = {}
+        xq = {}
+        o_tiles = {}
+        g1_tiles = {}
+        gq = {}
+
         def sort_words(b):
-            x_sorted = xs_pool.tile([P, TILES, CIN // 2], F32, name="x_sorted")
+            x_sorted[b] = xs_pool.tile([P, TILES, CIN // 2], F32, name="x_sorted_b")
             for half in range(2):
                 tiles = slice(2 * half, 2 * half + 2)
                 nc.scalar.copy(
-                    out=x_sorted[:, tiles, :].rearrange("p t (g u q) -> p (t g) u q", u=2, q=P),
+                    out=x_sorted[b][:, tiles, :].rearrange("p t (g u q) -> p (t g) u q", u=2, q=P),
                     in_=x_sb[b][:, tiles, :].bitcast(F32).rearrange("p t (g q u) -> p (t g) u q", u=2, q=P),
                 )
-            return x_sorted
 
         def words_of(b, t, g, u):
             if b in x_sorted:
                 return x_sorted[b][:, t, P * (2 * g + u) : P * (2 * g + u + 1)]
             return x_sb[b][:, t, :].bitcast(F32)[:, 2 * P * g + u : 2 * P * (g + 1) : 2]
 
-        def transpose_x(b, xg, part):
-            half, g = divmod(part, X_PASSES)
-            xt = psum_xt.tile([P, 2, HALF], F32, name="xt")
-            for tt in range(2):
-                for u in range(2):
-                    nc.tensor.transpose(xt[:, u, P * tt : P * (tt + 1)], words_of(b, 2 * half + tt, g, u), ident[:])
-            xg_words = xg[:, g, :].bitcast(F32).rearrange("p (n u) -> p n u", u=2)
-            nc.scalar.copy(
-                out=xg_words[:, HALF * half : HALF * (half + 1), :],
-                in_=xt[:].rearrange("p u n -> p n u"),
-            )
+        def transpose_x(b, parts=range(4)):
+            if b not in xg_tiles:
+                xg_tiles[b] = xg_pool.tile([P, X_PASSES, PACK * NODES], BF16, name="xg_b", align_bytes=64)
+            for part in parts:
+                half, g = divmod(part, X_PASSES)
+                xt = psum_xt.tile([P, 2, HALF], F32, name="xt")
+                for tt in range(2):
+                    for u in range(2):
+                        nc.tensor.transpose(
+                            xt[:, u, P * tt : P * (tt + 1)], words_of(b, 2 * half + tt, g, u), ident[:]
+                        )
+                xg_words = xg_tiles[b][:, g, :].bitcast(F32).rearrange("p (n u) -> p n u", u=2)
+                nc.scalar.copy(
+                    out=xg_words[:, HALF * half : HALF * (half + 1), :],
+                    in_=xt[:].rearrange("p u n -> p n u"),
+                )
 
-        def new_xg():
-            return xg_pool.tile([P, X_PASSES, PACK * NODES], BF16, name="xg", align_bytes=64)
-
-        def prepare_x(b):
-            xg = new_xg()
-            for part in range(4):
-                transpose_x(b, xg, part)
-            return quantise_x(xg)
-
-        def quantise_x(xg):
+        def new_xq(b):
             x_codes = xq_pool.tile([P, X_PASSES, NODES], U32, name="x_codes", align_bytes=64)
             x_scales = xq_pool.tile([P, X_PASSES, NODES], U8, name="x_scales", align_bytes=64)
+            xq[b] = (x_codes, x_scales)
+
+        def quantise_x(b):
+            new_xq(b)
+            x_codes, x_scales = xq[b]
             nc.vector.quantize_mx(
                 out=x_codes[:].rearrange("p g n -> p (g n)").bitcast(FP8X4),
                 scales=x_scales[:].rearrange("p g n -> p (g n)"),
-                in_=xg[:].rearrange("p g w -> p (g w)"),
+                in_=xg_tiles[b][:].rearrange("p g w -> p (g w)"),
             )
-            return x_codes, x_scales
 
-        def quantise_first_x(xg):
-            x_codes = xq_pool.tile([P, X_PASSES, NODES], U32, name="x_codes", align_bytes=64)
-            x_scales = xq_pool.tile([P, X_PASSES, NODES], U8, name="x_scales", align_bytes=64)
+        def quantise_x_by_parts(b):
+            new_xq(b)
+            x_codes, x_scales = xq[b]
             for half in range(2):
                 nodes = slice(HALF * half, HALF * (half + 1))
                 for g in range(X_PASSES):
                     nc.vector.quantize_mx(
                         out=x_codes[:, g, nodes].bitcast(FP8X4),
                         scales=x_scales[:, g, nodes],
-                        in_=xg[:, g, PACK * HALF * half : PACK * HALF * (half + 1)],
+                        in_=xg_tiles[b][:, g, PACK * HALF * half : PACK * HALF * (half + 1)],
                     )
-            return x_codes, x_scales
 
-        def project(acc, xq, t, which, c0, width):
-            x_codes, x_scales = xq
+        def project(acc, b, t, which, c0, width):
+            x_codes, x_scales = xq[b]
             nodes = slice(P * t, P * (t + 1))
             for g in range(X_PASSES):
                 wg = X_PASSES * which + g
@@ -179,143 +185,206 @@ def tile_modulatedgraphconv_pa_t_e_kernel(tc, x, W_words, W_scales, M, adj, adj2
                     stop=(g == X_PASSES - 1),
                 )
 
-        def self_term(b):
-            o_sb = o_pool.tile([P, TILES, COUT], F32, name="o_sb")
-            for t in range(TILES):
+        def self_term(b, tiles):
+            if b not in o_tiles:
+                o_tiles[b] = o_pool.tile([P, TILES, COUT], F32, name="o_sb_b")
+            for t in tiles:
+                o_t = o_tiles[b][:, t, :]
                 h0 = psum_acc.tile([P, COUT], F32, name="h0", tag="acc")
-                project(h0[:], xq[b], t, 0, 0, COUT)
-                if b == 0:
+                project(h0[:], b, t, 0, 0, COUT)
+                if b < 2:
                     nc.vector.scalar_tensor_tensor(
-                        out=o_sb[:, t, :],
-                        in0=h0[:],
-                        scalar=a_self[:, t : t + 1],
-                        in1=m_sb[:, t, :],
-                        op0=MULT,
-                        op1=MULT,
+                        out=o_t, in0=h0[:], scalar=a_self[:, t : t + 1], in1=m_sb[:, t, :], op0=MULT, op1=MULT
                     )
                 else:
-                    nc.vector.tensor_tensor(out=o_sb[:, t, :], in0=h0[:], in1=ms[:, t, :], op=MULT)
-                if t % 2 == 1:
-                    pair = o_sb[:, t - 1 : t + 1, :]
-                    nc.gpsimd.tensor_tensor(
-                        out=pair, in0=pair, in1=bias_all[:].unsqueeze(1).to_broadcast([P, 2, COUT]), op=ADD
-                    )
-            return o_sb
+                    nc.vector.tensor_tensor(out=o_t, in0=h0[:], in1=ms[:, t, :], op=MULT)
 
-        def neighbour_values(xq):
-            g1 = g_pool.tile([P, COUT, PACK], BF16, name="g1", align_bytes=64)
-            for s in range(COUT // P):
+        def add_bias(b, first, count):
+            o_part = o_tiles[b][:, first : first + count, :]
+            nc.gpsimd.tensor_tensor(
+                out=o_part, in0=o_part, in1=bias_all[:].unsqueeze(1).to_broadcast([P, count, COUT]), op=ADD
+            )
+
+        def neighbour_values(b, parts=range(COUT // P)):
+            if b not in g1_tiles:
+                g1_tiles[b] = g_pool.tile([P, COUT, PACK], BF16, name="g1_b", align_bytes=64)
+            for s in parts:
                 cols = slice(P * s, P * (s + 1))
                 h1 = psum_acc.tile([P, TILES, P], F32, name="h1", tag="acc")
                 for t in range(TILES):
-                    project(h1[:, t, :], xq, t, 1, P * s, P)
+                    project(h1[:, t, :], b, t, 1, P * s, P)
                 nc.vector.tensor_tensor(
-                    out=g1[:, cols, :], in0=h1[:].rearrange("p t c -> p c t"), in1=m_grouped[:, cols, :], op=MULT
+                    out=g1_tiles[b][:, cols, :],
+                    in0=h1[:].rearrange("p t c -> p c t"),
+                    in1=m_grouped[:, cols, :],
+                    op=MULT,
                 )
-            return g1
 
-        def quantise_neighbours(g1):
+        def quantise_neighbours(b):
             g_codes = g_pool.tile([P, COUT], U32, name="g_codes", align_bytes=64)
             g_scales = g_pool.tile([P, COUT], U8, name="g_scales", align_bytes=64)
+            gq[b] = (g_codes, g_scales)
             nc.vector.quantize_mx(
-                out=g_codes[:].bitcast(FP8X4), scales=g_scales[:], in_=g1[:].rearrange("p c t -> p (c t)")
+                out=g_codes[:].bitcast(FP8X4), scales=g_scales[:], in_=g1_tiles[b][:].rearrange("p c t -> p (c t)")
             )
-            return g_codes, g_scales
 
-        def aggregate_and_store(b, tiles=range(TILES)):
+        def aggregate(b, t):
             g_codes, g_scales = gq[b]
-            o_sb = o_tiles[b]
-            out_b = out[b].rearrange("(p t) c -> p t c", t=TILES)
-            for t in tiles:
-                nodes = slice(P * t, P * (t + 1))
-                agg = psum_acc.tile([P, COUT], F32, name="agg", tag="acc")
-                nc.tensor.matmul_mx(
-                    out=agg[:],
-                    lhsT=a_codes[:, nodes].bitcast(FP8X4),
-                    lhsT_scale=a_scales[:, nodes],
-                    rhs=g_codes[:].bitcast(FP8X4),
-                    rhs_scale=g_scales[:],
-                    start=True,
-                    stop=True,
-                )
-                nc.vector.tensor_tensor(out=o_sb[:, t, :], in0=agg[:], in1=o_sb[:, t, :], op=ADD)
-                nc.sync.dma_start(out=out_b[:, t, :], in_=o_sb[:, t, :])
+            nodes = slice(P * t, P * (t + 1))
+            agg = psum_acc.tile([P, COUT], F32, name="agg", tag="acc")
+            nc.tensor.matmul_mx(
+                out=agg[:],
+                lhsT=a_codes[:, nodes].bitcast(FP8X4),
+                lhsT_scale=a_scales[:, nodes],
+                rhs=g_codes[:].bitcast(FP8X4),
+                rhs_scale=g_scales[:],
+                start=True,
+                stop=True,
+            )
+            return agg
 
-        x_sorted = {}
-        xg = new_xg()
-        for part in range(4):
-            transpose_x(0, xg, part)
+        def store(b, t):
+            nc.sync.dma_start(out=out[b].rearrange("(p t) c -> p t c", t=TILES)[:, t, :], in_=o_tiles[b][:, t, :])
+
+        def finish(b, tiles):
+            for t in tiles:
+                agg = aggregate(b, t)
+                o_t = o_tiles[b][:, t, :]
+                nc.vector.tensor_tensor(out=o_t, in0=agg[:], in1=o_t, op=ADD)
+                store(b, t)
+
+        a_self = const.tile([P, TILES], F32)
+        ms = const.tile([P, TILES, COUT], F32)
+
+        def self_weights(tiles):
+            for t in tiles:
+                nc.scalar.activation(out=ms[:, t, :], in_=m_sb[:, t, :], func=COPY, scale=a_self[:, t : t + 1])
+
+        s = const.tile([P, TILES * TILES, P], F32)
+
+        def add_matrices():
+            nc.vector.tensor_tensor(
+                out=s[:].rearrange("p (t t2) m -> p t t2 m", t2=TILES),
+                in0=adj_sb[:].rearrange("p t (m t2) -> p t t2 m", t2=TILES),
+                in1=adj2_sb[:].rearrange("p t (m t2) -> p t t2 m", t2=TILES),
+                op=ADD,
+            )
+
+        def clear_diagonal():
+            diag_blocks = s[:, 0 : TILES * TILES : TILES + 1, :]
+            nc.vector.tensor_tensor(
+                out=diag_blocks,
+                in0=diag_blocks,
+                in1=off_diagonal[:].unsqueeze(1).to_broadcast([P, TILES, P]),
+                op=MULT,
+            )
+
+        a_grouped = const.tile([P, NODES, PACK], BF16, align_bytes=64)
+
+        def add_transpose():
+            flipped = {}
+            for t2 in range(TILES):
+                flipped[t2] = psum_acc.tile([P, TILES, P], F32, name="flipped_t2", tag="acc")
+                for t in range(TILES):
+                    nc.tensor.transpose(flipped[t2][:, t, :], s[:, TILES * t2 + t, :], ident[:])
+            for t2 in range(TILES):
+                nc.vector.tensor_tensor(
+                    out=a_grouped[:, P * t2 : P * (t2 + 1), :],
+                    in0=flipped[t2][:].rearrange("p t m -> p m t"),
+                    in1=s[:, t2 : TILES * TILES : TILES, :].rearrange("p t m -> p m t"),
+                    op=ADD,
+                )
+
+        a_codes = const.tile([P, NODES], U32, align_bytes=64)
+        a_scales = const.tile([P, NODES], U8, align_bytes=64)
+
+        def quantise_matrix():
+            nc.vector.quantize_mx(
+                out=a_codes[:].bitcast(FP8X4), scales=a_scales[:], in_=a_grouped[:].rearrange("p w t -> p (w t)")
+            )
+
+        transpose_x(0)
+        quantise_x_by_parts(0)
         bias_all = const.tile([P, COUT], BF16)
         spread = psum_acc.tile([P, COUT], F32, name="spread", tag="acc")
         nc.tensor.matmul(spread[:], lhsT=first_row[:], rhs=bias_row[:], start=True, stop=True)
         nc.scalar.copy(out=bias_all[:], in_=spread[:])
-
-        xq = {0: quantise_first_x(xg)}
-        a_self = const.tile([P, TILES], F32)
         nc.vector.tensor_tensor(out=a_self[:], in0=diag_adj[:], in1=diag_adj2[:], op=ADD)
         m_grouped = const.tile([P, COUT, PACK], BF16)
         for half in range(2):
             cols = slice(COUT // 2 * half, COUT // 2 * (half + 1))
             nc.scalar.mul(out=m_grouped[:, cols, :], in_=m_sb[:, :, cols].rearrange("p t c -> p c t"), mul=0.5)
-        ms = const.tile([P, TILES, COUT], F32)
-        for t in range(TILES):
-            nc.scalar.activation(out=ms[:, t, :], in_=m_sb[:, t, :], func=COPY, scale=a_self[:, t : t + 1])
-        o_tiles = {0: self_term(0)}
-        g1 = neighbour_values(xq[0])
-
-        s = const.tile([P, TILES * TILES, P], F32)
-        nc.vector.tensor_tensor(
-            out=s[:].rearrange("p (t t2) m -> p t t2 m", t2=TILES),
-            in0=adj_sb[:].rearrange("p t (m t2) -> p t t2 m", t2=TILES),
-            in1=adj2_sb[:].rearrange("p t (m t2) -> p t t2 m", t2=TILES),
-            op=ADD,
-        )
-        diag_blocks = s[:, 0 : TILES * TILES : TILES + 1, :]
-        nc.vector.tensor_tensor(
-            out=diag_blocks, in0=diag_blocks, in1=off_diagonal[:].unsqueeze(1).to_broadcast([P, TILES, P]), op=MULT
-        )
-        gq = {0: quantise_neighbours(g1)}
-        for b in range(1, AHEAD + 1):
-            xq[b] = prepare_x(b)
-        x_sorted[AHEAD + 1] = sort_words(AHEAD + 1)
+        self_term(0, range(2))
+        add_bias(0, 0, 2)
+        self_term(0, range(2, 3))
+        neighbour_values(0, range(3))
+        transpose_x(1, range(2))
+        add_matrices()
+        neighbour_values(0, range(3, 4))
+        clear_diagonal()
+        transpose_x(1, range(2, 4))
+        self_weights(range(2))
+        quantise_x(1)
+        transpose_x(2, range(1))
         for b in range(BATCH - 2, BATCH):
             load_x(b)
-        a_grouped = const.tile([P, NODES, PACK], BF16, align_bytes=64)
-        for t2 in range(TILES):
-            flipped = psum_acc.tile([P, TILES, P], F32, name="flipped", tag="acc")
-            for t in range(TILES):
-                nc.tensor.transpose(flipped[:, t, :], s[:, TILES * t2 + t, :], ident[:])
-            nc.vector.tensor_tensor(
-                out=a_grouped[:, P * t2 : P * (t2 + 1), :],
-                in0=flipped[:].rearrange("p t m -> p m t"),
-                in1=s[:, t2 : TILES * TILES : TILES, :].rearrange("p t m -> p m t"),
-                op=ADD,
-            )
-        a_codes = const.tile([P, NODES], U32, align_bytes=64)
-        a_scales = const.tile([P, NODES], U8, align_bytes=64)
-        nc.vector.quantize_mx(
-            out=a_codes[:].bitcast(FP8X4), scales=a_scales[:], in_=a_grouped[:].rearrange("p w t -> p (w t)")
-        )
+        self_term(0, range(3, 4))
+        add_bias(0, 2, 2)
+        quantise_neighbours(0)
+        self_weights(range(2, 4))
+        add_transpose()
+        transpose_x(2, range(1, 3))
+        neighbour_values(1, range(1))
+        self_term(1, range(1))
+        quantise_matrix()
+        neighbour_values(1, range(1, 2))
+        transpose_x(2, range(3, 4))
+        self_term(1, range(1, 2))
+        quantise_x(2)
+        add_bias(1, 0, 2)
+        self_term(1, range(2, 3))
+        neighbour_values(1, range(2, 4))
+        transpose_x(3)
+        finish(0, range(1))
+        self_term(1, range(3, 4))
+        add_bias(1, 2, 2)
+        finish(0, range(1, 4))
+        sort_words(4)
+        self_term(2, range(3))
+        quantise_x(3)
+        self_term(2, range(3, 4))
+        quantise_neighbours(1)
 
-        for b in range(1, BATCH - 1):
-            ahead = b + AHEAD
-            if ahead < BATCH:
-                xg = new_xg()
-                for part in range(4):
-                    transpose_x(ahead, xg, part)
-            o_tiles[b] = self_term(b)
-            aggregate_and_store(b - 1)
-            g1 = neighbour_values(xq[b])
-            if ahead < BATCH:
-                xq[ahead] = quantise_x(xg)
-            gq[b] = quantise_neighbours(g1)
-            if ahead + 1 < BATCH:
-                x_sorted[ahead + 1] = sort_words(ahead + 1)
-        last = BATCH - 1
-        o_tiles[last] = self_term(last)
-        aggregate_and_store(last - 1, range(2))
-        g1 = neighbour_values(xq[last])
-        aggregate_and_store(last - 1, range(2, 3))
-        gq[last] = quantise_neighbours(g1)
-        aggregate_and_store(last - 1, range(3, TILES))
-        aggregate_and_store(last)
+        for b in range(2, BATCH - 2):
+            neighbour_values(b)
+            transpose_x(b + 2)
+            finish(b - 1, range(TILES))
+            self_term(b + 1, range(3))
+            add_bias(b, 0, TILES)
+            quantise_x(b + 2)
+            self_term(b + 1, range(3, 4))
+            quantise_neighbours(b)
+            if b + 3 < BATCH:
+                sort_words(b + 3)
+
+        b = BATCH - 2
+        neighbour_values(b)
+        self_term(b + 1, range(3))
+        add_bias(b, 0, TILES)
+        finish(b - 1, range(1))
+        self_term(b + 1, range(3, 4))
+        quantise_neighbours(b)
+        add_bias(b + 1, 0, TILES)
+        finish(b - 1, range(1, 4))
+        finish(b, range(1))
+        neighbour_values(b + 1)
+        finish(b, range(1, 2))
+        quantise_neighbours(b + 1)
+        agg = aggregate(b, 3)
+        agg_sb = agg_pool.tile([P, COUT], F32)
+        nc.scalar.copy(out=agg_sb[:], in_=agg[:])
+        finish(b, range(2, 3))
+        o_t = o_tiles[b][:, 3, :]
+        nc.gpsimd.tensor_tensor(out=o_t, in0=agg_sb[:], in1=o_t, op=ADD)
+        store(b, 3)
+        finish(b + 1, range(TILES))

@@ -36,6 +36,7 @@ def tile_modulatedgraphconv_pa_t_e_kernel(tc, x, W_words, W_scales, M, adj, adj2
         xs_pool = ctx.enter_context(tc.tile_pool(name="xs_pool", bufs=2))
         xg_pool = ctx.enter_context(tc.tile_pool(name="xg_pool", bufs=2))
         xq_pool = ctx.enter_context(tc.tile_pool(name="xq_pool", bufs=AHEAD + 1))
+        gn_pool = ctx.enter_context(tc.tile_pool(name="gn_pool", bufs=2))
         g_pool = ctx.enter_context(tc.tile_pool(name="g_pool", bufs=2))
         o_pool = ctx.enter_context(tc.tile_pool(name="o_pool", bufs=BATCH))
         agg_pool = ctx.enter_context(tc.tile_pool(name="agg_pool", bufs=1))
@@ -110,6 +111,7 @@ def tile_modulatedgraphconv_pa_t_e_kernel(tc, x, W_words, W_scales, M, adj, adj2
         xg_tiles = {}
         xq = {}
         o_tiles = {}
+        g1_rows = {}
         g1_tiles = {}
         gq = {}
 
@@ -219,6 +221,19 @@ def tile_modulatedgraphconv_pa_t_e_kernel(tc, x, W_words, W_scales, M, adj, adj2
                     in1=m_grouped[:, cols, :],
                     op=MULT,
                 )
+
+        def neighbour_rows(b):
+            g1_rows[b] = gn_pool.tile([P, TILES, COUT], BF16, name="g1_rows_b")
+            for t in range(TILES):
+                h1 = psum_acc.tile([P, COUT], F32, name="h1", tag="acc")
+                project(h1[:], b, t, 1, 0, COUT)
+                nc.vector.scalar_tensor_tensor(
+                    out=g1_rows[b][:, t, :], in0=h1[:], scalar=0.5, in1=m_sb[:, t, :], op0=MULT, op1=MULT
+                )
+
+        def interleave_neighbours(b):
+            g1_tiles[b] = g_pool.tile([P, COUT, PACK], BF16, name="g1_b", align_bytes=64)
+            nc.scalar.copy(out=g1_tiles[b][:], in_=g1_rows[b][:].rearrange("p t c -> p c t"))
 
         def quantise_neighbours(b):
             g_codes = g_pool.tile([P, COUT], U32, name="g_codes", align_bytes=64)
@@ -356,8 +371,9 @@ def tile_modulatedgraphconv_pa_t_e_kernel(tc, x, W_words, W_scales, M, adj, adj2
         quantise_neighbours(1)
 
         for b in range(2, BATCH - 2):
-            neighbour_values(b)
+            neighbour_rows(b)
             transpose_x(b + 2)
+            interleave_neighbours(b)
             finish(b - 1, range(TILES))
             self_term(b + 1, range(3))
             add_bias(b, 0, TILES)

from contextlib import ExitStack

import concourse.mybir as mybir
from concourse.masks import make_identity

F32 = mybir.dt.float32
BF16 = mybir.dt.bfloat16
I32 = mybir.dt.int32
U32 = mybir.dt.uint32
U8 = mybir.dt.uint8
FP8X4 = mybir.dt.float8_e4m3fn_x4
ADD = mybir.AluOpType.add
MULT = mybir.AluOpType.mult
COPY = mybir.ActivationFunctionType.Copy

P = 128
PACK = 4
K_PASS = P * PACK
BATCH = 8
NODES = 512
CIN = 1024
COUT = 512
X_PASSES = CIN // K_PASS
TILES = NODES // P
HALF = NODES // 2
AHEAD = 2

FLOPS = 2 * BATCH * NODES * CIN * COUT * 2 + 2 * BATCH * NODES * NODES * COUT


def tile_modulatedgraphconv_pa_t_e_kernel(tc, x, W_words, W_scales, M, adj, adj2, bias, out):
    nc = tc.nc
    with ExitStack() as ctx:
        const = ctx.enter_context(tc.tile_pool(name="const", bufs=1))
        x_pool = ctx.enter_context(tc.tile_pool(name="x_pool", bufs=BATCH - 2))
        xs_pool = ctx.enter_context(tc.tile_pool(name="xs_pool", bufs=2))
        xg_pool = ctx.enter_context(tc.tile_pool(name="xg_pool", bufs=2))
        xq_pool = ctx.enter_context(tc.tile_pool(name="xq_pool", bufs=AHEAD + 1))
        gn_pool = ctx.enter_context(tc.tile_pool(name="gn_pool", bufs=2))
        g_pool = ctx.enter_context(tc.tile_pool(name="g_pool", bufs=2))
        o_pool = ctx.enter_context(tc.tile_pool(name="o_pool", bufs=BATCH))
        agg_pool = ctx.enter_context(tc.tile_pool(name="agg_pool", bufs=1))
        psum_xt = ctx.enter_context(tc.psum_pool(name="psum_xt", bufs=3))
        psum_acc = ctx.enter_context(tc.psum_pool(name="psum_acc", bufs=5))
        ctx.enter_context(tc.manual_schedule())

        diag_adj = const.tile([P, TILES], BF16)
        diag_adj2 = const.tile([P, TILES], BF16)
        with nc.allow_non_contiguous_dma(reason="the 512 diagonal elements of a matrix"):
            for diag_sb, matrix in ((diag_adj, adj), (diag_adj2, adj2)):
                nc.scalar.dma_start(
                    out=diag_sb[:],
                    in_=matrix.rearrange("i j -> (i j)")[0 : NODES * NODES : NODES + 1].rearrange(
                        "(p t) -> p t", t=TILES
                    ),
                )
        bias_row = const.tile([P, COUT], BF16)
        nc.vector.memset(bias_row[:], 0.0)
        first_row = const.tile([P, P], BF16)
        nc.vector.memset(first_row[:], 0.0)
        nc.vector.memset(first_row[0:1, :], 1.0)
        nc.scalar.dma_start(out=bias_row[0:1, :], in_=bias.unsqueeze(0))

        w_scales = const.tile([P, COUT], U8, align_bytes=64)
        nc.vector.memset(w_scales[:].bitcast(I32), 0)
        x_sb = {}

        def load_x(b):
            x_sb[b] = x_pool.tile([P, TILES, CIN], BF16, name="x_sb_b")
            x_b = x[b].rearrange("(p t) k -> p t k", t=TILES)
            for half in range(2):
                tiles = slice(2 * half, 2 * half + 2)
                nc.sync.dma_start(out=x_sb[b][:, tiles, :], in_=x_b[:, tiles, :])

        load_x(0)
        for quadrant in range(4):
            nc.sync.dma_start(
                out=w_scales[:].bitcast(I32)[32 * quadrant : 32 * quadrant + 4 * 2 * X_PASSES, :],
                in_=W_scales.bitcast(I32)[:, 4 * quadrant : 4 * quadrant + 4, :],
            )
        w_words = const.tile([P, 2 * X_PASSES, PACK * COUT], U8, align_bytes=64)

        def load_w(g):
            nc.sync.dma_start(
                out=w_words[:, g, :].bitcast(I32),
                in_=W_words[g].rearrange("p n t -> p (n t)").bitcast(I32),
            )

        load_w(0)
        load_w(1)
        m_sb = const.tile([P, TILES, COUT], BF16)
        nc.sync.dma_start(out=m_sb[:], in_=M.rearrange("(p t) c -> p t c", t=TILES))
        load_w(2)
        load_w(3)
        load_x(1)
        adj_sb = const.tile([P, TILES, NODES], BF16)
        adj2_sb = const.tile([P, TILES, NODES], BF16)
        nc.sync.dma_start(out=adj2_sb[:], in_=adj2.rearrange("(p t) i -> p t i", t=TILES))
        nc.sync.dma_start(out=adj_sb[:], in_=adj.rearrange("(p t) i -> p t i", t=TILES))
        for b in range(2, BATCH - 2):
            load_x(b)

        ident = const.tile([P, P], F32)
        make_identity(nc, ident[:])
        off_diagonal = const.tile([P, P], F32)
        nc.gpsimd.tensor_scalar(
            out=off_diagonal[:], in0=ident[:], scalar1=-1.0, scalar2=1.0, op0=MULT, op1=ADD
        )

        x_sorted = {}
        xg_tiles = {}
        xq = {}
        o_tiles = {}
        g1_rows = {}
        g1_tiles = {}
        gq = {}

        def sort_words(b):
            x_sorted[b] = xs_pool.tile([P, TILES, CIN // 2], F32, name="x_sorted_b")
            for half in range(2):
                tiles = slice(2 * half, 2 * half + 2)
                nc.scalar.copy(
                    out=x_sorted[b][:, tiles, :].rearrange("p t (g u q) -> p (t g) u q", u=2, q=P),
                    in_=x_sb[b][:, tiles, :].bitcast(F32).rearrange("p t (g q u) -> p (t g) u q", u=2, q=P),
                )

        def words_of(b, t, g, u):
            if b in x_sorted:
                return x_sorted[b][:, t, P * (2 * g + u) : P * (2 * g + u + 1)]
            return x_sb[b][:, t, :].bitcast(F32)[:, 2 * P * g + u : 2 * P * (g + 1) : 2]

        def transpose_x(b, parts=range(4)):
            if b not in xg_tiles:
                xg_tiles[b] = xg_pool.tile([P, X_PASSES, PACK * NODES], BF16, name="xg_b", align_bytes=64)
            for part in parts:
                half, g = divmod(part, X_PASSES)
                xt = psum_xt.tile([P, 2, HALF], F32, name="xt")
                for tt in range(2):
                    for u in range(2):
                        nc.tensor.transpose(
                            xt[:, u, P * tt : P * (tt + 1)], words_of(b, 2 * half + tt, g, u), ident[:]
                        )
                xg_words = xg_tiles[b][:, g, :].bitcast(F32).rearrange("p (n u) -> p n u", u=2)
                nc.scalar.copy(
                    out=xg_words[:, HALF * half : HALF * (half + 1), :],
                    in_=xt[:].rearrange("p u n -> p n u"),
                )

        def new_xq(b):
            x_codes = xq_pool.tile([P, X_PASSES, NODES], U32, name="x_codes", align_bytes=64)
            x_scales = xq_pool.tile([P, X_PASSES, NODES], U8, name="x_scales", align_bytes=64)
            xq[b] = (x_codes, x_scales)

        def quantise_x(b):
            new_xq(b)
            x_codes, x_scales = xq[b]
            nc.vector.quantize_mx(
                out=x_codes[:].rearrange("p g n -> p (g n)").bitcast(FP8X4),
                scales=x_scales[:].rearrange("p g n -> p (g n)"),
                in_=xg_tiles[b][:].rearrange("p g w -> p (g w)"),
            )

        def quantise_x_by_parts(b):
            new_xq(b)
            x_codes, x_scales = xq[b]
            for half in range(2):
                nodes = slice(HALF * half, HALF * (half + 1))
                for g in range(X_PASSES):
                    nc.vector.quantize_mx(
                        out=x_codes[:, g, nodes].bitcast(FP8X4),
                        scales=x_scales[:, g, nodes],
                        in_=xg_tiles[b][:, g, PACK * HALF * half : PACK * HALF * (half + 1)],
                    )

        def project(acc, b, t, which, c0, width):
            x_codes, x_scales = xq[b]
            nodes = slice(P * t, P * (t + 1))
            for g in range(X_PASSES):
                wg = X_PASSES * which + g
                nc.tensor.matmul_mx(
                    out=acc,
                    lhsT=x_codes[:, g, nodes].bitcast(FP8X4),
                    lhsT_scale=x_scales[:, g, nodes],
                    rhs=w_words[:, wg, PACK * c0 : PACK * (c0 + width)].bitcast(FP8X4),
                    rhs_scale=w_scales[4 * wg : P, c0 : c0 + width],
                    start=(g == 0),
                    stop=(g == X_PASSES - 1),
                )

        def self_term(b, tiles):
            if b not in o_tiles:
                o_tiles[b] = o_pool.tile([P, TILES, COUT], F32, name="o_sb_b")
            for t in tiles:
                o_t = o_tiles[b][:, t, :]
                h0 = psum_acc.tile([P, COUT], F32, name="h0", tag="acc")
                project(h0[:], b, t, 0, 0, COUT)
                if b < 2:
                    nc.vector.scalar_tensor_tensor(
                        out=o_t, in0=h0[:], scalar=a_self[:, t : t + 1], in1=m_sb[:, t, :], op0=MULT, op1=MULT
                    )
                else:
                    nc.vector.tensor_tensor(out=o_t, in0=h0[:], in1=ms[:, t, :], op=MULT)

        def add_bias(b, first, count):
            o_part = o_tiles[b][:, first : first + count, :]
            nc.gpsimd.tensor_tensor(
                out=o_part, in0=o_part, in1=bias_all[:].unsqueeze(1).to_broadcast([P, count, COUT]), op=ADD
            )

        def neighbour_values(b, parts=range(COUT // P)):
            if b not in g1_tiles:
                g1_tiles[b] = g_pool.tile([P, COUT, PACK], BF16, name="g1_b", align_bytes=64)
            for s in parts:
                cols = slice(P * s, P * (s + 1))
                h1 = psum_acc.tile([P, TILES, P], F32, name="h1", tag="acc")
                for t in range(TILES):
                    project(h1[:, t, :], b, t, 1, P * s, P)
                nc.vector.tensor_tensor(
                    out=g1_tiles[b][:, cols, :],
                    in0=h1[:].rearrange("p t c -> p c t"),
                    in1=m_grouped[:, cols, :],
                    op=MULT,
                )

        def neighbour_rows(b):
            g1_rows[b] = gn_pool.tile([P, TILES, COUT], BF16, name="g1_rows_b")
            for t in range(TILES):
                h1 = psum_acc.tile([P, COUT], F32, name="h1", tag="acc")
                project(h1[:], b, t, 1, 0, COUT)
                nc.vector.scalar_tensor_tensor(
                    out=g1_rows[b][:, t, :], in0=h1[:], scalar=0.5, in1=m_sb[:, t, :], op0=MULT, op1=MULT
                )

        def interleave_neighbours(b):
            g1_tiles[b] = g_pool.tile([P, COUT, PACK], BF16, name="g1_b", align_bytes=64)
            nc.scalar.copy(out=g1_tiles[b][:], in_=g1_rows[b][:].rearrange("p t c -> p c t"))

        def quantise_neighbours(b):
            g_codes = g_pool.tile([P, COUT], U32, name="g_codes", align_bytes=64)
            g_scales = g_pool.tile([P, COUT], U8, name="g_scales", align_bytes=64)
            gq[b] = (g_codes, g_scales)
            nc.vector.quantize_mx(
                out=g_codes[:].bitcast(FP8X4), scales=g_scales[:], in_=g1_tiles[b][:].rearrange("p c t -> p (c t)")
            )

        def aggregate(b, t):
            g_codes, g_scales = gq[b]
            nodes = slice(P * t, P * (t + 1))
            agg = psum_acc.tile([P, COUT], F32, name="agg", tag="acc")
            nc.tensor.matmul_mx(
                out=agg[:],
                lhsT=a_codes[:, nodes].bitcast(FP8X4),
                lhsT_scale=a_scales[:, nodes],
                rhs=g_codes[:].bitcast(FP8X4),
                rhs_scale=g_scales[:],
                start=True,
                stop=True,
            )
            return agg

        def store(b, t):
            nc.sync.dma_start(out=out[b].rearrange("(p t) c -> p t c", t=TILES)[:, t, :], in_=o_tiles[b][:, t, :])

        def finish(b, tiles):
            for t in tiles:
                agg = aggregate(b, t)
                o_t = o_tiles[b][:, t, :]
                nc.vector.tensor_tensor(out=o_t, in0=agg[:], in1=o_t, op=ADD)
                store(b, t)

        a_self = const.tile([P, TILES], F32)
        ms = const.tile([P, TILES, COUT], F32)

        def self_weights(tiles):
            for t in tiles:
                nc.scalar.activation(out=ms[:, t, :], in_=m_sb[:, t, :], func=COPY, scale=a_self[:, t : t + 1])

        s = const.tile([P, TILES * TILES, P], F32)

        def add_matrices():
            nc.vector.tensor_tensor(
                out=s[:].rearrange("p (t t2) m -> p t t2 m", t2=TILES),
                in0=adj_sb[:].rearrange("p t (m t2) -> p t t2 m", t2=TILES),
                in1=adj2_sb[:].rearrange("p t (m t2) -> p t t2 m", t2=TILES),
                op=ADD,
            )

        def clear_diagonal():
            diag_blocks = s[:, 0 : TILES * TILES : TILES + 1, :]
            nc.vector.tensor_tensor(
                out=diag_blocks,
                in0=diag_blocks,
                in1=off_diagonal[:].unsqueeze(1).to_broadcast([P, TILES, P]),
                op=MULT,
            )

        a_grouped = const.tile([P, NODES, PACK], BF16, align_bytes=64)

        def add_transpose():
            flipped = {}
            for t2 in range(TILES):
                flipped[t2] = psum_acc.tile([P, TILES, P], F32, name="flipped_t2", tag="acc")
                for t in range(TILES):
                    nc.tensor.transpose(flipped[t2][:, t, :], s[:, TILES * t2 + t, :], ident[:])
            for t2 in range(TILES):
                nc.vector.tensor_tensor(
                    out=a_grouped[:, P * t2 : P * (t2 + 1), :],
                    in0=flipped[t2][:].rearrange("p t m -> p m t"),
                    in1=s[:, t2 : TILES * TILES : TILES, :].rearrange("p t m -> p m t"),
                    op=ADD,
                )

        a_codes = const.tile([P, NODES], U32, align_bytes=64)
        a_scales = const.tile([P, NODES], U8, align_bytes=64)

        def quantise_matrix():
            nc.vector.quantize_mx(
                out=a_codes[:].bitcast(FP8X4), scales=a_scales[:], in_=a_grouped[:].rearrange("p w t -> p (w t)")
            )

        transpose_x(0)
        quantise_x_by_parts(0)
        bias_all = const.tile([P, COUT], BF16)
        spread = psum_acc.tile([P, COUT], F32, name="spread", tag="acc")
        nc.tensor.matmul(spread[:], lhsT=first_row[:], rhs=bias_row[:], start=True, stop=True)
        nc.scalar.copy(out=bias_all[:], in_=spread[:])
        nc.vector.tensor_tensor(out=a_self[:], in0=diag_adj[:], in1=diag_adj2[:], op=ADD)
        m_grouped = const.tile([P, COUT, PACK], BF16)
        for half in range(2):
            cols = slice(COUT // 2 * half, COUT // 2 * (half + 1))
            nc.scalar.mul(out=m_grouped[:, cols, :], in_=m_sb[:, :, cols].rearrange("p t c -> p c t"), mul=0.5)
        self_term(0, range(2))
        add_bias(0, 0, 2)
        self_term(0, range(2, 3))
        neighbour_values(0, range(3))
        transpose_x(1, range(2))
        add_matrices()
        neighbour_values(0, range(3, 4))
        clear_diagonal()
        transpose_x(1, range(2, 4))
        self_weights(range(2))
        quantise_x(1)
        transpose_x(2, range(1))
        for b in range(BATCH - 2, BATCH):
            load_x(b)
        self_term(0, range(3, 4))
        add_bias(0, 2, 2)
        quantise_neighbours(0)
        self_weights(range(2, 4))
        add_transpose()
        transpose_x(2, range(1, 3))
        neighbour_values(1, range(1))
        self_term(1, range(1))
        quantise_matrix()
        neighbour_values(1, range(1, 2))
        transpose_x(2, range(3, 4))
        self_term(1, range(1, 2))
        quantise_x(2)
        add_bias(1, 0, 2)
        self_term(1, range(2, 3))
        neighbour_values(1, range(2, 4))
        transpose_x(3)
        finish(0, range(1))
        self_term(1, range(3, 4))
        add_bias(1, 2, 2)
        finish(0, range(1, 4))
        sort_words(4)
        self_term(2, range(3))
        quantise_x(3)
        self_term(2, range(3, 4))
        quantise_neighbours(1)

        for b in range(2, BATCH - 2):
            neighbour_rows(b)
            transpose_x(b + 2)
            interleave_neighbours(b)
            finish(b - 1, range(TILES))
            self_term(b + 1, range(3))
            add_bias(b, 0, TILES)
            quantise_x(b + 2)
            self_term(b + 1, range(3, 4))
            quantise_neighbours(b)
            if b + 3 < BATCH:
                sort_words(b + 3)

        b = BATCH - 2
        neighbour_values(b)
        self_term(b + 1, range(3))
        add_bias(b, 0, TILES)
        finish(b - 1, range(1))
        self_term(b + 1, range(3, 4))
        quantise_neighbours(b)
        add_bias(b + 1, 0, TILES)
        finish(b - 1, range(1, 4))
        finish(b, range(1))
        neighbour_values(b + 1)
        finish(b, range(1, 2))
        quantise_neighbours(b + 1)
        agg = aggregate(b, 3)
        agg_sb = agg_pool.tile([P, COUT], F32)
        nc.scalar.copy(out=agg_sb[:], in_=agg[:])
        finish(b, range(2, 3))
        o_t = o_tiles[b][:, 3, :]
        nc.gpsimd.tensor_tensor(out=o_t, in0=agg_sb[:], in1=o_t, op=ADD)
        store(b, 3)
        finish(b + 1, range(TILES))
